import numpy as np
import ml_dtypes


def mxq(x, axis, fmt="e4m3"):
    dtype, down = {"e4m3": (ml_dtypes.float8_e4m3fn, 7), "e5m2": (ml_dtypes.float8_e5m2, 14)}[fmt]
    v = np.moveaxis(np.asarray(x, np.float32).astype(ml_dtypes.bfloat16).astype(np.float64), axis, -1)
    blocks = v.reshape(v.shape[:-1] + (-1, 32))
    amax = np.abs(blocks).max(-1, keepdims=True)
    byte = np.maximum(np.where(amax > 0, np.frexp(amax)[1] - 1 + 127, 0) - down, 1)
    scale = np.exp2(byte - 127.0)
    codes = (blocks / scale).astype(np.float32).astype(dtype).astype(np.float64)
    return np.moveaxis((codes * scale).reshape(v.shape), -1, axis)


WIDE = False


def mx_kscale(k):
    if not WIDE:
        return np.ones(k)
    levels = np.array([30, -30])
    if k % 512:
        return np.exp2(np.random.permutation(np.resize(levels, k // 32))).repeat(32)
    a = np.empty((k // 512, 16))
    for p in range(k // 512):
        a[p, :8] = np.random.permutation(np.resize(levels, 8))
        for g in range(8):
            far = levels[np.abs(levels - a[p, g]) >= 10]
            a[p, g + 8] = far[np.random.randint(len(far))]
    return np.exp2(a.ravel()).repeat(32)


BF16 = ml_dtypes.bfloat16


def bf(x):
    return np.asarray(x, np.float32).astype(BF16)


def f64(x):
    return np.asarray(x).astype(np.float64)


B, S, D, NQ, NKV, H, WINDOW, QB = 1, 1024, 1024, 8, 4, 256, 512, 512
HALF = H // 2
MAX_WAVELENGTH = 10000.0


def rope_interleaved(u):
    inv_freq = 1.0 / MAX_WAVELENGTH ** (np.arange(0, H, 2) / H)
    freq = np.arange(S)[:, None] * inv_freq[None, :]
    cos = np.cos(freq)[None, :, None, :]
    sin = np.sin(freq)[None, :, None, :]
    u1, u2 = u[..., :HALF], u[..., HALF:]
    r1 = u1 * cos - u2 * sin
    r2 = u2 * cos + u1 * sin
    return np.stack([r1, r2], axis=-1).reshape(u.shape)


def setup_inputs():
    s = mx_kscale(D)
    return {"x": bf(np.random.standard_normal((B, S, D)) * s),
            "Wq": bf(np.random.standard_normal((NQ, D, H)) * 2.5 / np.sqrt(D) / s[None, :, None]),
            "Wk": bf(np.random.standard_normal((NKV, D, H)) * 2.5 / np.sqrt(D) / s[None, :, None])}


def reference(x, Wq, Wk):
    xq = mxq(f64(x), 2, "e5m2")
    uq = (xq[:, None] @ mxq(f64(Wq), 1, "e5m2")[None]).transpose(0, 2, 1, 3)
    uk = (xq[:, None] @ mxq(f64(Wk), 1, "e5m2")[None]).transpose(0, 2, 1, 3)
    q = rope_interleaved(uq) * (1.0 / np.sqrt(H))
    k = rope_interleaved(uk)
    return q, k

@@ -1,0 +1,298 @@
+import math
+from contextlib import ExitStack
+
+import concourse.mybir as mybir
+from concourse.masks import make_identity
+
+F32 = mybir.dt.float32
+BF16 = mybir.dt.bfloat16
+U32 = mybir.dt.uint32
+U8 = mybir.dt.uint8
+I32 = mybir.dt.int32
+FP8X4 = mybir.dt.float8_e5m2_x4
+ALU = mybir.AluOpType
+ACT = mybir.ActivationFunctionType
+
+P = 128
+S_TOK = 1024
+D_MODEL = 1024
+H = 256
+HALF = 128
+NT = S_TOK // P
+NPASS = D_MODEL // 512
+NG = 6
+LOOKAHEAD = 5
+FLOPS = 2 * S_TOK * D_MODEL * 12 * H
+CHUNKS = [(0, 2), (2, 4), (4, 8)]
+
+
+def tile_gemma2attention_pa_kernel(tc, x, Wq, Wk, out_0, out_1):
+    nc = tc.nc
+    groups = [(Wk, out_1, 0, False), (Wk, out_1, 2, False),
+              (Wq, out_0, 0, True), (Wq, out_0, 2, True), (Wq, out_0, 4, True), (Wq, out_0, 6, True)]
+    total = NG * NT
+
+    with ExitStack() as ctx:
+        keep = ctx.enter_context(tc.tile_pool(name="keep", bufs=1))
+        stage = ctx.enter_context(tc.tile_pool(name="stage", bufs=4))
+        psum = ctx.enter_context(tc.psum_pool(name="psum", bufs=8))
+        ctx.enter_context(tc.manual_schedule())
+
+        xr = {}
+        wr = {}
+
+        def load_x(t):
+            tl = keep.tile([P, D_MODEL], BF16, name="xr%d" % t)
+            nc.sync.dma_start(out=tl[:], in_=x[0, t * P:(t + 1) * P, :])
+            xr[t] = tl
+
+        def load_w(g, c):
+            src = groups[g][0]
+            h0 = groups[g][2]
+            tl = keep.tile([P, 2, 4, H], BF16, name="wr%d_%d" % (g, c))
+            nc.sync.dma_start(
+                out=tl[:],
+                in_=src[h0:h0 + 2, c * 512:(c + 1) * 512, :].rearrange("h (p j) w -> p h j w", j=4))
+            wr[(g, c)] = tl
+
+        load_w(0, 0)
+        load_x(0)
+        load_w(0, 1)
+        for t in range(1, NT):
+            load_x(t)
+        for g in range(1, NG):
+            load_w(g, 0)
+            load_w(g, 1)
+
+        ang = keep.tile([P, NT, HALF], F32, name="ang")
+        nc.gpsimd.iota(ang[:, :, 0], pattern=[[P, NT]], base=0, channel_multiplier=1,
+                       allow_small_or_imprecise_dtypes=True)
+        ident = keep.tile([P, P], F32, name="ident")
+        make_identity(nc, ident[:])
+        junk = keep.tile([P, 2], F32, name="junk")
+        nc.vector.memset(junk[:, 0:1], 0.0)
+        nc.scalar.activation(out=junk[:, 1:2], in_=junk[:, 0:1], func=ACT.Sin)
+
+        ratio = 10000.0 ** (-1.0 / HALF)
+        k = 1
+        while k < HALF:
+            nc.vector.tensor_scalar(out=ang[:, :, k:2 * k], in0=ang[:, :, 0:k], scalar1=ratio ** k,
+                                    scalar2=None, op0=ALU.mult)
+            k *= 2
+
+        red = {}
+        tabs = {}
+        tabqs = {}
+
+        def reduce_angle(key, t0, t1):
+            n = t1 - t0
+            a = ang[:, t0:t1, :]
+            ti = keep.tile([P, n, HALF], I32, name="ti%d" % key)
+            nc.vector.tensor_scalar(out=ti[:], in0=a, scalar1=1.0 / (2.0 * math.pi),
+                                    scalar2=None, op0=ALU.mult)
+            tf = keep.tile([P, n, HALF], F32, name="tf%d" % key)
+            nc.vector.tensor_copy(out=tf[:], in_=ti[:])
+            r = keep.tile([P, n, HALF], F32, name="red%d" % key)
+            nc.vector.scalar_tensor_tensor(out=r[:].rearrange("p t i -> p (t i)"),
+                                           in0=tf[:].rearrange("p t i -> p (t i)"),
+                                           scalar=-2.0 * math.pi,
+                                           in1=a.rearrange("p t i -> p (t i)"),
+                                           op0=ALU.mult, op1=ALU.add)
+            red[key] = r
+
+        def trig(ci, key, off):
+            t0, t1 = CHUNKS[ci]
+            n = t1 - t0
+            r = red[key][:, off:off + n, :]
+            tb = keep.tile([P, 3, n, HALF], F32, name="tab%d" % ci)
+            ab = keep.tile([P, n, HALF], F32, name="abs%d" % ci)
+            nc.scalar.activation(out=tb[:, 2, :, :], in_=r, func=ACT.Sin)
+            nc.scalar.activation(out=ab[:], in_=r, func=ACT.Abs)
+            nc.scalar.activation(out=tb[:, 1, :, :], in_=ab[:], func=ACT.Sin, scale=-1.0, bias=math.pi / 2.0)
+            nc.gpsimd.tensor_scalar(out=tb[:, 0, :, :], in0=tb[:, 2, :, :], scalar1=-1.0, scalar2=0.0,
+                                    op0=ALU.mult, op1=ALU.add)
+            tabs[ci] = tb
+
+        def scale_tables():
+            for ci in range(len(CHUNKS)):
+                t0, t1 = CHUNKS[ci]
+                tq = keep.tile([P, 3, t1 - t0, HALF], F32, name="tabq%d" % ci)
+                nc.scalar.activation(out=tq[:], in_=tabs[ci][:], func=ACT.Copy, scale=1.0 / 16.0)
+                tabqs[ci] = tq
+
+        def table_of(t, scaled):
+            for ci in range(len(CHUNKS)):
+                t0, t1 = CHUNKS[ci]
+                if t0 <= t < t1:
+                    return (tabqs[ci] if scaled else tabs[ci]), t - t0
+            return None, 0
+
+        xt_ps = {}
+        xg_sb = {}
+        xc = {}
+        xs = {}
+        wg_sb = {}
+        wc = {}
+        ws = {}
+        acc_ps = {}
+        p_sb = {}
+        q_sb = {}
+
+        def x_transpose(t):
+            words = xr[t][:].bitcast(F32)
+            xt = psum.tile([P, NPASS, 2, P], F32, tag="bank", name="xt")
+            for c in range(NPASS):
+                for u in range(2):
+                    nc.tensor.transpose(xt[:, c, u, :], words[:, 256 * c + u:256 * (c + 1):2], ident[:])
+            xt_ps[t] = xt
+
+        def x_evac(t):
+            xg = stage.tile([P, NPASS * P * 4], BF16, tag="xg", bufs=8, name="xg", align_bytes=64)
+            nc.scalar.copy(out=xg[:].bitcast(F32).rearrange("p (c r u) -> p c r u", c=NPASS, u=2),
+                           in_=xt_ps[t][:].rearrange("p c u r -> p c r u"))
+            xg_sb[t] = xg
+
+        def x_quant(t):
+            codes = keep.tile([P, NPASS * P], U32, name="xc%d" % t, align_bytes=64)
+            scales = keep.tile([P, NPASS * P], U8, name="xs%d" % t, align_bytes=64)
+            nc.vector.quantize_mx(out=codes[:].bitcast(FP8X4), scales=scales[:], in_=xg_sb[t][:])
+            xc[t] = codes
+            xs[t] = scales
+
+        def w_inter(g, c, eng):
+            wg = stage.tile([P, 2048], BF16, tag="wg", bufs=4, name="wg", align_bytes=64)
+            dst = wg[:].rearrange("p (h w j) -> p h w j", h=2, j=4)
+            src = wr[(g, c)][:].rearrange("p h j w -> p h w j")
+            if eng == "v":
+                nc.vector.tensor_copy(out=dst, in_=src)
+            else:
+                nc.scalar.copy(out=dst, in_=src)
+            wg_sb[(g, c)] = wg
+
+        def w_quant(g, c):
+            codes = keep.tile([P, 512], U32, name="wc%d_%d" % (g, c), align_bytes=64)
+            scales = keep.tile([P, 512], U8, name="ws%d_%d" % (g, c), align_bytes=64)
+            nc.vector.quantize_mx(out=codes[:].bitcast(FP8X4), scales=scales[:], in_=wg_sb[(g, c)][:])
+            wc[(g, c)] = codes
+            ws[(g, c)] = scales
+
+        def mm(n):
+            g, t = divmod(n, NT)
+            acc = psum.tile([P, 512], F32, tag="bank", name="acc")
+            for c in range(NPASS):
+                nc.tensor.matmul_mx(out=acc[:],
+                                    lhsT=xc[t][:, c * P:(c + 1) * P].bitcast(FP8X4),
+                                    lhsT_scale=xs[t][:, c * P:(c + 1) * P],
+                                    rhs=wc[(g, c)][:].bitcast(FP8X4),
+                                    rhs_scale=ws[(g, c)][:],
+                                    start=(c == 0), stop=(c == NPASS - 1))
+            acc_ps[n] = acc
+
+        def rope_mul(n):
+            g, t = divmod(n, NT)
+            table, tl = table_of(t, groups[g][3])
+            accv = acc_ps[n][:].rearrange("p (h f i) -> p h f i", h=2, f=2)
+            shape = [P, 2, HALF, 2]
+            a = n % 2
+            if a == 0:
+                pt_new = stage.tile([P, 2, 512], F32, tag="pt", bufs=4, name="pt")
+                qt_new = stage.tile([P, 2, 512], F32, tag="qt", bufs=3, name="qt")
+                p_sb[n // 2] = pt_new
+                q_sb[n // 2] = qt_new
+            pt = p_sb[n // 2]
+            qt = q_sb[n // 2]
+            nc.vector.tensor_tensor(
+                out=pt[:, a, :].rearrange("p (h i e) -> p h i e", h=2, e=2),
+                in0=accv[:, :, 0, :].unsqueeze(3).to_broadcast(shape),
+                in1=table[:, 1:3, tl, :].rearrange("p e i -> p i e").unsqueeze(1).to_broadcast(shape),
+                op=ALU.mult)
+            nc.vector.tensor_tensor(
+                out=qt[:, a, :].rearrange("p (h i e) -> p h i e", h=2, e=2),
+                in0=accv[:, :, 1, :].unsqueeze(3).to_broadcast(shape),
+                in1=table[:, 0:2, tl, :].rearrange("p e i -> p i e").unsqueeze(1).to_broadcast(shape),
+                op=ALU.mult)
+
+        def add_store(n, count, eng):
+            g, t = divmod(n, NT)
+            dst = groups[g][1]
+            h0 = groups[g][2]
+            a = n % 2
+            pt = p_sb[n // 2][:, a:a + count, :]
+            qt = q_sb[n // 2][:, a:a + count, :]
+            if eng == "v":
+                nc.vector.tensor_tensor(out=pt, in0=pt, in1=qt, op=ALU.add)
+            else:
+                nc.gpsimd.tensor_tensor(out=pt, in0=pt, in1=qt, op=ALU.add)
+            nc.sync.dma_start(
+                out=dst[0, t * P:(t + count) * P, h0:h0 + 2, :].rearrange("(a p) h d -> p a h d", p=P),
+                in_=pt.rearrange("p a (h d) -> p a h d", h=2))
+
+        reduce_angle(0, 0, 2)
+        trig(0, 0, 0)
+        reduce_angle(1, 2, 8)
+        w_inter(0, 0, "v")
+        x_transpose(0)
+        x_evac(0)
+        w_inter(0, 1, "s")
+        x_transpose(1)
+        x_evac(1)
+        trig(1, 1, 0)
+        x_transpose(2)
+        x_evac(2)
+        w_quant(0, 0)
+        x_quant(0)
+        w_quant(0, 1)
+        x_quant(1)
+        mm(0)
+        x_transpose(3)
+        x_evac(3)
+        x_transpose(4)
+        x_evac(4)
+        trig(2, 1, 2)
+        mm(1)
+        x_transpose(5)
+        x_evac(5)
+        x_transpose(6)
+        x_evac(6)
+
+        done_mm = [2]
+        ready_groups = [1]
+
+        def matmuls_up_to(limit):
+            while done_mm[0] < min(limit, total, ready_groups[0] * NT):
+                mm(done_mm[0])
+                done_mm[0] += 1
+
+        for n in range(total):
+            g, t = divmod(n, NT)
+            if g > 0:
+                if g + 1 < NG and t in (2, 3):
+                    w_quant(g + 1, t - 2)
+                    if g + 3 < NG:
+                        w_inter(g + 3, t - 2, "s")
+                    if t == 3:
+                        ready_groups[0] = g + 2
+                matmuls_up_to(n + LOOKAHEAD + 1)
+            rope_mul(n)
+            if n >= total - 2:
+                add_store(n, 1, "g" if n == total - 2 else "v")
+            elif n % 2 == 1:
+                add_store(n - 1, 2, "g")
+            if g == 0:
+                if t + 2 < NT:
+                    x_quant(t + 2)
+                    matmuls_up_to(t + 3)
+                if t == 0:
+                    x_transpose(7)
+                    x_evac(7)
+                    w_inter(1, 0, "s")
+                    w_inter(1, 1, "s")
+                    w_inter(2, 0, "s")
+                    w_inter(2, 1, "s")
+                    scale_tables()
+                if t in (5, 6):
+                    w_quant(1, t - 5)
+                    w_inter(3, t - 5, "s")
+                    if t == 6:
+                        ready_groups[0] = 2
+                        matmuls_up_to(n + LOOKAHEAD + 1)

@@ -21,16 +21,15 @@ HALF = 128
 NT = S_TOK // P
 NPASS = D_MODEL // 512
 NG = 6
-LOOKAHEAD = 5
 FLOPS = 2 * S_TOK * D_MODEL * 12 * H
 CHUNKS = [(0, 2), (2, 4), (4, 8)]
+SCHEDULE = [('loadw', 0, 0), ('loadx', 0), ('loadw', 0, 1), ('loadx', 1), ('loadx', 2), ('loadx', 3), ('loadx', 4), ('loadx', 5), ('loadx', 6), ('loadx', 7), ('loadw', 1, 0), ('loadw', 1, 1), ('loadw', 2, 0), ('loadw', 2, 1), ('loadw', 3, 0), ('loadw', 3, 1), ('loadw', 4, 0), ('loadw', 4, 1), ('loadw', 5, 0), ('loadw', 5, 1), ('const',), ('red', 0, 2), ('trig', 0, 0, 2), ('red', 1, 6), ('wint', 0, 0, 'v'), ('xT', 0), ('xev', 0), ('wint', 0, 1, 's'), ('xT', 1), ('xev', 1), ('trig', 1, 1, 2), ('xT', 2), ('xev', 2), ('wq', 0, 0), ('xq', 0), ('wq', 0, 1), ('xq', 1), ('mm', 0), ('xT', 3), ('xev', 3), ('xT', 4), ('xev', 4), ('trig', 2, 1, 4), ('mm', 1), ('xT', 5), ('xev', 5), ('xT', 6), ('xev', 6), ('P', 0), ('Q', 0), ('xq2', 2), ('mm', 2), ('mm', 3), ('xT', 7), ('xev', 7), ('wint', 1, 0, 's'), ('wint', 1, 1, 's'), ('wint', 2, 0, 's'), ('wint', 2, 1, 's'), ('tabq',), ('P', 1), ('Q', 1), ('add', 0, 2, 'g'), ('P', 2), ('Q', 2), ('xq2', 4), ('mm', 4), ('mm', 5), ('P', 3), ('Q', 3), ('add', 2, 2, 'g'), ('P', 4), ('Q', 4), ('xq2', 6), ('mm', 6), ('mm', 7), ('P', 5), ('Q', 5), ('add', 4, 2, 'g'), ('wq2', 1), ('wint', 3, 0, 's'), ('wint', 3, 1, 's'), ('mm', 8), ('mm', 9), ('mm', 10), ('P', 6), ('Q', 6), ('P', 7), ('Q', 7), ('add', 6, 2, 'g'), ('mm', 11), ('mm', 12), ('mm', 13), ('P', 8), ('Q', 8), ('mm', 14), ('P', 9), ('Q', 9), ('add', 8, 2, 'g'), ('mm', 15), ('P', 10), ('Q', 10), ('P', 11), ('Q', 11), ('add', 10, 2, 'g'), ('wq2', 2), ('wint', 4, 0, 's'), ('wint', 4, 1, 's'), ('mm', 16), ('mm', 17), ('P', 12), ('Q', 12), ('mm', 18), ('P', 13), ('Q', 13), ('add', 12, 2, 'g'), ('mm', 19), ('P', 14), ('Q', 14), ('mm', 20), ('P', 15), ('Q', 15), ('add', 14, 2, 'g'), ('mm', 21), ('P', 16), ('Q', 16), ('mm', 22), ('P', 17), ('Q', 17), ('add', 16, 2, 'g'), ('mm', 23), ('P', 18), ('Q', 18), ('P', 19), ('Q', 19), ('add', 18, 2, 'g'), ('wq2', 3), ('wint', 5, 0, 's'), ('wint', 5, 1, 's'), ('mm', 24), ('mm', 25), ('P', 20), ('Q', 20), ('mm', 26), ('P', 21), ('Q', 21), ('add', 20, 2, 'g'), ('mm', 27), ('P', 22), ('Q', 22), ('mm', 28), ('P', 23), ('Q', 23), ('add', 22, 2, 'g'), ('mm', 29), ('P', 24), ('Q', 24), ('mm', 30), ('P', 25), ('Q', 25), ('add', 24, 2, 'g'), ('mm', 31), ('P', 26), ('Q', 26), ('P', 27), ('Q', 27), ('add', 26, 2, 'g'), ('wq2', 4), ('mm', 32), ('mm', 33), ('P', 28), ('Q', 28), ('mm', 34), ('P', 29), ('Q', 29), ('add', 28, 2, 'g'), ('mm', 35), ('P', 30), ('Q', 30), ('mm', 36), ('P', 31), ('Q', 31), ('add', 30, 2, 'g'), ('mm', 37), ('P', 32), ('Q', 32), ('mm', 38), ('P', 33), ('Q', 33), ('add', 32, 2, 'g'), ('mm', 39), ('P', 34), ('Q', 34), ('P', 35), ('Q', 35), ('add', 34, 2, 'g'), ('wq2', 5), ('mm', 40), ('mm', 41), ('P', 36), ('Q', 36), ('mm', 42), ('P', 37), ('Q', 37), ('add', 36, 2, 'g'), ('mm', 43), ('P', 38), ('Q', 38), ('mm', 44), ('P', 39), ('Q', 39), ('add', 38, 2, 'g'), ('mm', 45), ('P', 40), ('Q', 40), ('mm', 46), ('P', 41), ('Q', 41), ('add', 40, 2, 'g'), ('mm', 47), ('P', 42), ('Q', 42), ('P', 43), ('Q', 43), ('add', 42, 2, 'g'), ('P', 44), ('Q', 44), ('P', 45), ('Q', 45), ('add', 44, 2, 'g'), ('P', 46), ('Q', 46), ('add', 46, 1, 'g'), ('P', 47), ('Q', 47), ('add', 47, 1, 'v')]
 
 
 def tile_gemma2attention_pa_kernel(tc, x, Wq, Wk, out_0, out_1):
     nc = tc.nc
     groups = [(Wk, out_1, 0, False), (Wk, out_1, 2, False),
               (Wq, out_0, 0, True), (Wq, out_0, 2, True), (Wq, out_0, 4, True), (Wq, out_0, 6, True)]
-    total = NG * NT
 
     with ExitStack() as ctx:
         keep = ctx.enter_context(tc.tile_pool(name="keep", bufs=1))
@@ -40,6 +39,20 @@ def tile_gemma2attention_pa_kernel(tc, x, Wq, Wk, out_0, out_1):
 
         xr = {}
         wr = {}
+        red = {}
+        tabs = {}
+        tabqs = {}
+        xt_ps = {}
+        xg_sb = {}
+        xc = {}
+        xs = {}
+        wg_sb = {}
+        wc = {}
+        ws = {}
+        acc_ps = {}
+        p_sb = {}
+        q_sb = {}
+        misc = {}
 
         def load_x(t):
             tl = keep.tile([P, D_MODEL], BF16, name="xr%d" % t)
@@ -55,38 +68,27 @@ def tile_gemma2attention_pa_kernel(tc, x, Wq, Wk, out_0, out_1):
                 in_=src[h0:h0 + 2, c * 512:(c + 1) * 512, :].rearrange("h (p j) w -> p h j w", j=4))
             wr[(g, c)] = tl
 
-        load_w(0, 0)
-        load_x(0)
-        load_w(0, 1)
-        for t in range(1, NT):
-            load_x(t)
-        for g in range(1, NG):
-            load_w(g, 0)
-            load_w(g, 1)
+        def const():
+            ang = keep.tile([P, NT, HALF], F32, name="ang")
+            nc.gpsimd.iota(ang[:, :, 0], pattern=[[P, NT]], base=0, channel_multiplier=1,
+                           allow_small_or_imprecise_dtypes=True)
+            ident = keep.tile([P, P], F32, name="ident")
+            make_identity(nc, ident[:])
+            junk = keep.tile([P, 2], F32, name="junk")
+            nc.vector.memset(junk[:, 0:1], 0.0)
+            nc.scalar.activation(out=junk[:, 1:2], in_=junk[:, 0:1], func=ACT.Sin)
+            ratio = 10000.0 ** (-1.0 / HALF)
+            k = 1
+            while k < HALF:
+                nc.vector.tensor_scalar(out=ang[:, :, k:2 * k], in0=ang[:, :, 0:k], scalar1=ratio ** k,
+                                        scalar2=None, op0=ALU.mult)
+                k *= 2
+            misc["ang"] = ang
+            misc["ident"] = ident
 
-        ang = keep.tile([P, NT, HALF], F32, name="ang")
-        nc.gpsimd.iota(ang[:, :, 0], pattern=[[P, NT]], base=0, channel_multiplier=1,
-                       allow_small_or_imprecise_dtypes=True)
-        ident = keep.tile([P, P], F32, name="ident")
-        make_identity(nc, ident[:])
-        junk = keep.tile([P, 2], F32, name="junk")
-        nc.vector.memset(junk[:, 0:1], 0.0)
-        nc.scalar.activation(out=junk[:, 1:2], in_=junk[:, 0:1], func=ACT.Sin)
-
-        ratio = 10000.0 ** (-1.0 / HALF)
-        k = 1
-        while k < HALF:
-            nc.vector.tensor_scalar(out=ang[:, :, k:2 * k], in0=ang[:, :, 0:k], scalar1=ratio ** k,
-                                    scalar2=None, op0=ALU.mult)
-            k *= 2
-
-        red = {}
-        tabs = {}
-        tabqs = {}
-
-        def reduce_angle(key, t0, t1):
-            n = t1 - t0
-            a = ang[:, t0:t1, :]
+        def reduce_angle(key, n):
+            t0 = 0 if key == 0 else 2
+            a = misc["ang"][:, t0:t0 + n, :]
             ti = keep.tile([P, n, HALF], I32, name="ti%d" % key)
             nc.vector.tensor_scalar(out=ti[:], in0=a, scalar1=1.0 / (2.0 * math.pi),
                                     scalar2=None, op0=ALU.mult)
@@ -100,9 +102,8 @@ def tile_gemma2attention_pa_kernel(tc, x, Wq, Wk, out_0, out_1):
                                            op0=ALU.mult, op1=ALU.add)
             red[key] = r
 
-        def trig(ci, key, off):
-            t0, t1 = CHUNKS[ci]
-            n = t1 - t0
+        def trig(ci, key, n):
+            off = 2 if ci == 2 else 0
             r = red[key][:, off:off + n, :]
             tb = keep.tile([P, 3, n, HALF], F32, name="tab%d" % ci)
             ab = keep.tile([P, n, HALF], F32, name="abs%d" % ci)
@@ -127,90 +128,92 @@ def tile_gemma2attention_pa_kernel(tc, x, Wq, Wk, out_0, out_1):
                     return (tabqs[ci] if scaled else tabs[ci]), t - t0
             return None, 0
 
-        xt_ps = {}
-        xg_sb = {}
-        xc = {}
-        xs = {}
-        wg_sb = {}
-        wc = {}
-        ws = {}
-        acc_ps = {}
-        p_sb = {}
-        q_sb = {}
-
         def x_transpose(t):
             words = xr[t][:].bitcast(F32)
             xt = psum.tile([P, NPASS, 2, P], F32, tag="bank", name="xt")
             for c in range(NPASS):
                 for u in range(2):
-                    nc.tensor.transpose(xt[:, c, u, :], words[:, 256 * c + u:256 * (c + 1):2], ident[:])
+                    nc.tensor.transpose(xt[:, c, u, :], words[:, 256 * c + u:256 * (c + 1):2], misc["ident"][:])
             xt_ps[t] = xt
 
         def x_evac(t):
-            xg = stage.tile([P, NPASS * P * 4], BF16, tag="xg", bufs=8, name="xg", align_bytes=64)
-            nc.scalar.copy(out=xg[:].bitcast(F32).rearrange("p (c r u) -> p c r u", c=NPASS, u=2),
+            if t % 2 == 0:
+                xg_new = stage.tile([P, 2, 1024], BF16, tag="xg", bufs=4, name="xg", align_bytes=64)
+                xg_sb[t // 2] = xg_new
+                xc_new = keep.tile([P, 2, 256], U32, name="xc%d" % (t // 2), align_bytes=64)
+                xs_new = keep.tile([P, 2, 256], U8, name="xs%d" % (t // 2), align_bytes=64)
+                xc[t // 2] = xc_new
+                xs[t // 2] = xs_new
+            nc.scalar.copy(out=xg_sb[t // 2][:, t % 2, :].bitcast(F32).rearrange("p (c r u) -> p c r u", c=NPASS, u=2),
                            in_=xt_ps[t][:].rearrange("p c u r -> p c r u"))
-            xg_sb[t] = xg
 
         def x_quant(t):
-            codes = keep.tile([P, NPASS * P], U32, name="xc%d" % t, align_bytes=64)
-            scales = keep.tile([P, NPASS * P], U8, name="xs%d" % t, align_bytes=64)
-            nc.vector.quantize_mx(out=codes[:].bitcast(FP8X4), scales=scales[:], in_=xg_sb[t][:])
-            xc[t] = codes
-            xs[t] = scales
+            nc.vector.quantize_mx(out=xc[t // 2][:, t % 2, :].bitcast(FP8X4), scales=xs[t // 2][:, t % 2, :],
+                                  in_=xg_sb[t // 2][:, t % 2, :])
+
+        def x_quant2(t):
+            nc.vector.quantize_mx(out=xc[t // 2][:].rearrange("p a n -> p (a n)").bitcast(FP8X4),
+                                  scales=xs[t // 2][:].rearrange("p a n -> p (a n)"),
+                                  in_=xg_sb[t // 2][:].rearrange("p a n -> p (a n)"))
 
         def w_inter(g, c, eng):
-            wg = stage.tile([P, 2048], BF16, tag="wg", bufs=4, name="wg", align_bytes=64)
-            dst = wg[:].rearrange("p (h w j) -> p h w j", h=2, j=4)
+            if c == 0:
+                wg_new = stage.tile([P, 2, 2048], BF16, tag="wg", bufs=3, name="wg", align_bytes=64)
+                wg_sb[g] = wg_new
+                wc_new = keep.tile([P, 2, 512], U32, name="wc%d" % g, align_bytes=64)
+                ws_new = keep.tile([P, 2, 512], U8, name="ws%d" % g, align_bytes=64)
+                wc[g] = wc_new
+                ws[g] = ws_new
+            dst = wg_sb[g][:, c, :].rearrange("p (h w j) -> p h w j", h=2, j=4)
             src = wr[(g, c)][:].rearrange("p h j w -> p h w j")
             if eng == "v":
                 nc.vector.tensor_copy(out=dst, in_=src)
             else:
                 nc.scalar.copy(out=dst, in_=src)
-            wg_sb[(g, c)] = wg
 
         def w_quant(g, c):
-            codes = keep.tile([P, 512], U32, name="wc%d_%d" % (g, c), align_bytes=64)
-            scales = keep.tile([P, 512], U8, name="ws%d_%d" % (g, c), align_bytes=64)
-            nc.vector.quantize_mx(out=codes[:].bitcast(FP8X4), scales=scales[:], in_=wg_sb[(g, c)][:])
-            wc[(g, c)] = codes
-            ws[(g, c)] = scales
+            nc.vector.quantize_mx(out=wc[g][:, c, :].bitcast(FP8X4), scales=ws[g][:, c, :], in_=wg_sb[g][:, c, :])
+
+        def w_quant2(g):
+            nc.vector.quantize_mx(out=wc[g][:].rearrange("p a n -> p (a n)").bitcast(FP8X4),
+                                  scales=ws[g][:].rearrange("p a n -> p (a n)"),
+                                  in_=wg_sb[g][:].rearrange("p a n -> p (a n)"))
 
         def mm(n):
             g, t = divmod(n, NT)
             acc = psum.tile([P, 512], F32, tag="bank", name="acc")
             for c in range(NPASS):
                 nc.tensor.matmul_mx(out=acc[:],
-                                    lhsT=xc[t][:, c * P:(c + 1) * P].bitcast(FP8X4),
-                                    lhsT_scale=xs[t][:, c * P:(c + 1) * P],
-                                    rhs=wc[(g, c)][:].bitcast(FP8X4),
-                                    rhs_scale=ws[(g, c)][:],
+                                    lhsT=xc[t // 2][:, t % 2, c * P:(c + 1) * P].bitcast(FP8X4),
+                                    lhsT_scale=xs[t // 2][:, t % 2, c * P:(c + 1) * P],
+                                    rhs=wc[g][:, c, :].bitcast(FP8X4),
+                                    rhs_scale=ws[g][:, c, :],
                                     start=(c == 0), stop=(c == NPASS - 1))
             acc_ps[n] = acc
 
-        def rope_mul(n):
+        def rope_half(n, f):
             g, t = divmod(n, NT)
             table, tl = table_of(t, groups[g][3])
             accv = acc_ps[n][:].rearrange("p (h f i) -> p h f i", h=2, f=2)
             shape = [P, 2, HALF, 2]
             a = n % 2
-            if a == 0:
+            if a == 0 and f == 0:
                 pt_new = stage.tile([P, 2, 512], F32, tag="pt", bufs=4, name="pt")
                 qt_new = stage.tile([P, 2, 512], F32, tag="qt", bufs=3, name="qt")
                 p_sb[n // 2] = pt_new
                 q_sb[n // 2] = qt_new
-            pt = p_sb[n // 2]
-            qt = q_sb[n // 2]
+            dst = p_sb[n // 2] if f == 0 else q_sb[n // 2]
             nc.vector.tensor_tensor(
-                out=pt[:, a, :].rearrange("p (h i e) -> p h i e", h=2, e=2),
-                in0=accv[:, :, 0, :].unsqueeze(3).to_broadcast(shape),
-                in1=table[:, 1:3, tl, :].rearrange("p e i -> p i e").unsqueeze(1).to_broadcast(shape),
+                out=dst[:, a, :].rearrange("p (h i e) -> p h i e", h=2, e=2),
+                in0=accv[:, :, f, :].unsqueeze(3).to_broadcast(shape),
+                in1=table[:, 1 - f:3 - f, tl, :].rearrange("p e i -> p i e").unsqueeze(1).to_broadcast(shape),
                 op=ALU.mult)
-            nc.vector.tensor_tensor(
-                out=qt[:, a, :].rearrange("p (h i e) -> p h i e", h=2, e=2),
-                in0=accv[:, :, 1, :].unsqueeze(3).to_broadcast(shape),
-                in1=table[:, 0:2, tl, :].rearrange("p e i -> p i e").unsqueeze(1).to_broadcast(shape),
-                op=ALU.mult)
+
+        def rope_p(n):
+            rope_half(n, 0)
+
+        def rope_q(n):
+            rope_half(n, 1)
 
         def add_store(n, count, eng):
             g, t = divmod(n, NT)
@@ -227,72 +230,9 @@ def tile_gemma2attention_pa_kernel(tc, x, Wq, Wk, out_0, out_1):
                 out=dst[0, t * P:(t + count) * P, h0:h0 + 2, :].rearrange("(a p) h d -> p a h d", p=P),
                 in_=pt.rearrange("p a (h d) -> p a h d", h=2))
 
-        reduce_angle(0, 0, 2)
-        trig(0, 0, 0)
-        reduce_angle(1, 2, 8)
-        w_inter(0, 0, "v")
-        x_transpose(0)
-        x_evac(0)
-        w_inter(0, 1, "s")
-        x_transpose(1)
-        x_evac(1)
-        trig(1, 1, 0)
-        x_transpose(2)
-        x_evac(2)
-        w_quant(0, 0)
-        x_quant(0)
-        w_quant(0, 1)
-        x_quant(1)
-        mm(0)
-        x_transpose(3)
-        x_evac(3)
-        x_transpose(4)
-        x_evac(4)
-        trig(2, 1, 2)
-        mm(1)
-        x_transpose(5)
-        x_evac(5)
-        x_transpose(6)
-        x_evac(6)
-
-        done_mm = [2]
-        ready_groups = [1]
-
-        def matmuls_up_to(limit):
-            while done_mm[0] < min(limit, total, ready_groups[0] * NT):
-                mm(done_mm[0])
-                done_mm[0] += 1
-
-        for n in range(total):
-            g, t = divmod(n, NT)
-            if g > 0:
-                if g + 1 < NG and t in (2, 3):
-                    w_quant(g + 1, t - 2)
-                    if g + 3 < NG:
-                        w_inter(g + 3, t - 2, "s")
-                    if t == 3:
-                        ready_groups[0] = g + 2
-                matmuls_up_to(n + LOOKAHEAD + 1)
-            rope_mul(n)
-            if n >= total - 2:
-                add_store(n, 1, "g" if n == total - 2 else "v")
-            elif n % 2 == 1:
-                add_store(n - 1, 2, "g")
-            if g == 0:
-                if t + 2 < NT:
-                    x_quant(t + 2)
-                    matmuls_up_to(t + 3)
-                if t == 0:
-                    x_transpose(7)
-                    x_evac(7)
-                    w_inter(1, 0, "s")
-                    w_inter(1, 1, "s")
-                    w_inter(2, 0, "s")
-                    w_inter(2, 1, "s")
-                    scale_tables()
-                if t in (5, 6):
-                    w_quant(1, t - 5)
-                    w_inter(3, t - 5, "s")
-                    if t == 6:
-                        ready_groups[0] = 2
-                        matmuls_up_to(n + LOOKAHEAD + 1)
+        stages = {"loadw": load_w, "loadx": load_x, "const": const, "red": reduce_angle, "trig": trig,
+                  "tabq": scale_tables, "xT": x_transpose, "xev": x_evac, "xq": x_quant, "xq2": x_quant2,
+                  "wint": w_inter, "wq": w_quant, "wq2": w_quant2, "mm": mm, "P": rope_p, "Q": rope_q,
+                  "add": add_store}
+        for step in SCHEDULE:
+            stages[step[0]](*step[1:])

@@ -23,7 +23,7 @@ NPASS = D_MODEL // 512
 NG = 6
 FLOPS = 2 * S_TOK * D_MODEL * 12 * H
 CHUNKS = [(0, 2), (2, 4), (4, 8)]
-SCHEDULE = [('loadw', 0, 0), ('loadx', 0), ('loadw', 0, 1), ('loadx', 1), ('loadx', 2), ('loadx', 3), ('loadx', 4), ('loadx', 5), ('loadx', 6), ('loadx', 7), ('loadw', 1, 0), ('loadw', 1, 1), ('loadw', 2, 0), ('loadw', 2, 1), ('loadw', 3, 0), ('loadw', 3, 1), ('loadw', 4, 0), ('loadw', 4, 1), ('loadw', 5, 0), ('loadw', 5, 1), ('const',), ('red', 0, 2), ('trig', 0, 0, 2), ('red', 1, 6), ('wint', 0, 0, 'v'), ('xT', 0), ('xev', 0), ('wint', 0, 1, 's'), ('xT', 1), ('xev', 1), ('trig', 1, 1, 2), ('xT', 2), ('xev', 2), ('wq', 0, 0), ('xq', 0), ('wq', 0, 1), ('xq', 1), ('mm', 0), ('xT', 3), ('xev', 3), ('xT', 4), ('xev', 4), ('trig', 2, 1, 4), ('mm', 1), ('xT', 5), ('xev', 5), ('xT', 6), ('xev', 6), ('P', 0), ('Q', 0), ('xq2', 2), ('mm', 2), ('mm', 3), ('xT', 7), ('xev', 7), ('wint', 1, 0, 's'), ('wint', 1, 1, 's'), ('wint', 2, 0, 's'), ('wint', 2, 1, 's'), ('tabq',), ('P', 1), ('Q', 1), ('add', 0, 2, 'g'), ('P', 2), ('Q', 2), ('xq2', 4), ('mm', 4), ('mm', 5), ('P', 3), ('Q', 3), ('add', 2, 2, 'g'), ('P', 4), ('Q', 4), ('xq2', 6), ('mm', 6), ('mm', 7), ('P', 5), ('Q', 5), ('add', 4, 2, 'g'), ('wq2', 1), ('wint', 3, 0, 's'), ('wint', 3, 1, 's'), ('mm', 8), ('mm', 9), ('mm', 10), ('P', 6), ('Q', 6), ('P', 7), ('Q', 7), ('add', 6, 2, 'g'), ('mm', 11), ('mm', 12), ('mm', 13), ('P', 8), ('Q', 8), ('mm', 14), ('P', 9), ('Q', 9), ('add', 8, 2, 'g'), ('mm', 15), ('P', 10), ('Q', 10), ('P', 11), ('Q', 11), ('add', 10, 2, 'g'), ('wq2', 2), ('wint', 4, 0, 's'), ('wint', 4, 1, 's'), ('mm', 16), ('mm', 17), ('P', 12), ('Q', 12), ('mm', 18), ('P', 13), ('Q', 13), ('add', 12, 2, 'g'), ('mm', 19), ('P', 14), ('Q', 14), ('mm', 20), ('P', 15), ('Q', 15), ('add', 14, 2, 'g'), ('mm', 21), ('P', 16), ('Q', 16), ('mm', 22), ('P', 17), ('Q', 17), ('add', 16, 2, 'g'), ('mm', 23), ('P', 18), ('Q', 18), ('P', 19), ('Q', 19), ('add', 18, 2, 'g'), ('wq2', 3), ('wint', 5, 0, 's'), ('wint', 5, 1, 's'), ('mm', 24), ('mm', 25), ('P', 20), ('Q', 20), ('mm', 26), ('P', 21), ('Q', 21), ('add', 20, 2, 'g'), ('mm', 27), ('P', 22), ('Q', 22), ('mm', 28), ('P', 23), ('Q', 23), ('add', 22, 2, 'g'), ('mm', 29), ('P', 24), ('Q', 24), ('mm', 30), ('P', 25), ('Q', 25), ('add', 24, 2, 'g'), ('mm', 31), ('P', 26), ('Q', 26), ('P', 27), ('Q', 27), ('add', 26, 2, 'g'), ('wq2', 4), ('mm', 32), ('mm', 33), ('P', 28), ('Q', 28), ('mm', 34), ('P', 29), ('Q', 29), ('add', 28, 2, 'g'), ('mm', 35), ('P', 30), ('Q', 30), ('mm', 36), ('P', 31), ('Q', 31), ('add', 30, 2, 'g'), ('mm', 37), ('P', 32), ('Q', 32), ('mm', 38), ('P', 33), ('Q', 33), ('add', 32, 2, 'g'), ('mm', 39), ('P', 34), ('Q', 34), ('P', 35), ('Q', 35), ('add', 34, 2, 'g'), ('wq2', 5), ('mm', 40), ('mm', 41), ('P', 36), ('Q', 36), ('mm', 42), ('P', 37), ('Q', 37), ('add', 36, 2, 'g'), ('mm', 43), ('P', 38), ('Q', 38), ('mm', 44), ('P', 39), ('Q', 39), ('add', 38, 2, 'g'), ('mm', 45), ('P', 40), ('Q', 40), ('mm', 46), ('P', 41), ('Q', 41), ('add', 40, 2, 'g'), ('mm', 47), ('P', 42), ('Q', 42), ('P', 43), ('Q', 43), ('add', 42, 2, 'g'), ('P', 44), ('Q', 44), ('P', 45), ('Q', 45), ('add', 44, 2, 'g'), ('P', 46), ('Q', 46), ('add', 46, 1, 'g'), ('P', 47), ('Q', 47), ('add', 47, 1, 'v')]
+SCHEDULE = [('loadw', 0, 0), ('loadx', 0), ('loadw', 0, 1), ('loadx', 1), ('loadx', 2), ('loadx', 3), ('loadx', 4), ('loadx', 5), ('loadx', 6), ('loadx', 7), ('loadw', 1, 0), ('loadw', 1, 1), ('loadw', 2, 0), ('loadw', 2, 1), ('loadw', 3, 0), ('loadw', 3, 1), ('loadw', 4, 0), ('loadw', 4, 1), ('loadw', 5, 0), ('loadw', 5, 1), ('const',), ('red', 0, 2), ('trig', 0, 0, 2), ('red', 1, 6), ('wint', 0, 0, 'v'), ('xT', 0), ('xev', 0), ('wint', 0, 1, 's'), ('xT', 1), ('xev', 1), ('trig', 1, 1, 2), ('xT', 2), ('xev', 2), ('wq', 0, 0), ('xq', 0), ('wq', 0, 1), ('xq', 1), ('xT', 3), ('xev', 3), ('xT', 4), ('xev', 4), ('trig', 2, 1, 4), ('xT', 5), ('xev', 5), ('xT', 6), ('xev', 6), ('mm', 0), ('mm', 1), ('P', 0), ('Q', 0), ('xq2', 2), ('mm', 2), ('xT', 7), ('xev', 7), ('wint', 1, 0, 's'), ('wint', 1, 1, 's'), ('wint', 2, 0, 's'), ('wint', 2, 1, 's'), ('tabq',), ('P', 1), ('Q', 1), ('add', 0, 2, 'g'), ('mm', 3), ('P', 2), ('Q', 2), ('xq2', 4), ('mm', 4), ('P', 3), ('Q', 3), ('add', 2, 2, 'g'), ('mm', 5), ('P', 4), ('Q', 4), ('xq2', 6), ('mm', 6), ('P', 5), ('Q', 5), ('add', 4, 2, 'g'), ('wq2', 1), ('mm', 7), ('mm', 8), ('mm', 9), ('wint', 3, 0, 's'), ('wint', 3, 1, 's'), ('P', 6), ('Q', 6), ('P', 7), ('Q', 7), ('add', 6, 2, 'g'), ('mm', 10), ('mm', 11), ('mm', 12), ('P', 8), ('Q', 8), ('add', 8, 1, 'g'), ('mm', 13), ('P', 9), ('Q', 9), ('add', 9, 1, 'pe'), ('mm', 14), ('P', 10), ('Q', 10), ('mm', 15), ('P', 11), ('Q', 11), ('add', 10, 2, 'g'), ('wq2', 2), ('wint', 4, 0, 's'), ('wint', 4, 1, 's'), ('mm', 16), ('P', 12), ('Q', 12), ('add', 12, 1, 'g'), ('mm', 17), ('P', 13), ('Q', 13), ('add', 13, 1, 'pe'), ('mm', 18), ('P', 14), ('Q', 14), ('mm', 19), ('P', 15), ('Q', 15), ('add', 14, 2, 'g'), ('mm', 20), ('P', 16), ('Q', 16), ('add', 16, 1, 'g'), ('mm', 21), ('P', 17), ('Q', 17), ('add', 17, 1, 'pe'), ('mm', 22), ('P', 18), ('Q', 18), ('mm', 23), ('P', 19), ('Q', 19), ('add', 18, 2, 'g'), ('wq2', 3), ('wint', 5, 0, 's'), ('wint', 5, 1, 's'), ('mm', 24), ('P', 20), ('Q', 20), ('add', 20, 1, 'g'), ('mm', 25), ('P', 21), ('Q', 21), ('add', 21, 1, 'pe'), ('mm', 26), ('P', 22), ('Q', 22), ('mm', 27), ('P', 23), ('Q', 23), ('add', 22, 2, 'g'), ('mm', 28), ('P', 24), ('Q', 24), ('add', 24, 1, 'g'), ('mm', 29), ('P', 25), ('Q', 25), ('add', 25, 1, 'pe'), ('mm', 30), ('P', 26), ('Q', 26), ('mm', 31), ('P', 27), ('Q', 27), ('add', 26, 2, 'g'), ('wq2', 4), ('mm', 32), ('P', 28), ('Q', 28), ('add', 28, 1, 'g'), ('mm', 33), ('P', 29), ('Q', 29), ('add', 29, 1, 'pe'), ('mm', 34), ('P', 30), ('Q', 30), ('mm', 35), ('P', 31), ('Q', 31), ('add', 30, 2, 'g'), ('mm', 36), ('P', 32), ('Q', 32), ('add', 32, 1, 'g'), ('mm', 37), ('P', 33), ('Q', 33), ('add', 33, 1, 'pe'), ('mm', 38), ('P', 34), ('Q', 34), ('mm', 39), ('P', 35), ('Q', 35), ('add', 34, 2, 'g'), ('wq2', 5), ('mm', 40), ('P', 36), ('Q', 36), ('add', 36, 1, 'g'), ('mm', 41), ('P', 37), ('Q', 37), ('add', 37, 1, 'pe'), ('mm', 42), ('P', 38), ('Q', 38), ('mm', 43), ('P', 39), ('Q', 39), ('add', 38, 2, 'g'), ('mm', 44), ('P', 40), ('Q', 40), ('add', 40, 1, 'g'), ('mm', 45), ('P', 41), ('Q', 41), ('add', 41, 1, 'pe'), ('mm', 46), ('P', 42), ('Q', 42), ('mm', 47), ('P', 43), ('Q', 43), ('add', 42, 2, 'g'), ('P', 44), ('Q', 44), ('add', 44, 1, 'g'), ('P', 45), ('Q', 45), ('add', 45, 1, 'pe'), ('P', 46), ('Q', 46), ('P', 47), ('Q', 47), ('add', 46, 1, 'v'), ('add', 47, 1, 'v')]
 
 
 def tile_gemma2attention_pa_kernel(tc, x, Wq, Wk, out_0, out_1):
@@ -224,6 +224,11 @@ def tile_gemma2attention_pa_kernel(tc, x, Wq, Wk, out_0, out_1):
             qt = q_sb[n // 2][:, a:a + count, :]
             if eng == "v":
                 nc.vector.tensor_tensor(out=pt, in0=pt, in1=qt, op=ALU.add)
+            elif eng == "pe":
+                bank = psum.tile([P, 512], F32, tag="bank", name="sumbank")
+                nc.tensor.matmul(out=bank[:], lhsT=misc["ident"][:], rhs=p_sb[n // 2][:, a, :], start=True, stop=False)
+                nc.tensor.matmul(out=bank[:], lhsT=misc["ident"][:], rhs=q_sb[n // 2][:, a, :], start=False, stop=True)
+                nc.scalar.copy(out=p_sb[n // 2][:, a, :], in_=bank[:])
             else:
                 nc.gpsimd.tensor_tensor(out=pt, in0=pt, in1=qt, op=ALU.add)
             nc.sync.dma_start(

@@ -14,16 +14,28 @@ ALU = mybir.AluOpType
 ACT = mybir.ActivationFunctionType
 
 P = 128
-S_TOK = 1024
-D_MODEL = 1024
-H = 256
-HALF = 128
-NT = S_TOK // P
-NPASS = D_MODEL // 512
-NG = 6
-FLOPS = 2 * S_TOK * D_MODEL * 12 * H
-CHUNKS = [(0, 2), (2, 4), (4, 8)]
-SCHEDULE = [('loadw', 0, 0), ('loadx', 0), ('loadw', 0, 1), ('loadx', 1), ('loadx', 2), ('loadx', 3), ('loadx', 4), ('loadx', 5), ('loadx', 6), ('loadx', 7), ('loadw', 1, 0), ('loadw', 1, 1), ('loadw', 2, 0), ('loadw', 2, 1), ('loadw', 3, 0), ('loadw', 3, 1), ('loadw', 4, 0), ('loadw', 4, 1), ('loadw', 5, 0), ('loadw', 5, 1), ('const',), ('red', 0, 2), ('trig', 0, 0, 2), ('red', 1, 6), ('wint', 0, 0, 'v'), ('xT', 0), ('xev', 0), ('wint', 0, 1, 's'), ('xT', 1), ('xev', 1), ('trig', 1, 1, 2), ('xT', 2), ('xev', 2), ('wq', 0, 0), ('xq', 0), ('wq', 0, 1), ('xq', 1), ('xT', 3), ('xev', 3), ('xT', 4), ('xev', 4), ('trig', 2, 1, 4), ('xT', 5), ('xev', 5), ('xT', 6), ('xev', 6), ('mm', 0), ('mm', 1), ('P', 0), ('Q', 0), ('xq2', 2), ('mm', 2), ('xT', 7), ('xev', 7), ('wint', 1, 0, 's'), ('wint', 1, 1, 's'), ('wint', 2, 0, 's'), ('wint', 2, 1, 's'), ('tabq',), ('P', 1), ('Q', 1), ('add', 0, 2, 'g'), ('mm', 3), ('P', 2), ('Q', 2), ('xq2', 4), ('mm', 4), ('P', 3), ('Q', 3), ('add', 2, 2, 'g'), ('mm', 5), ('P', 4), ('Q', 4), ('xq2', 6), ('mm', 6), ('P', 5), ('Q', 5), ('add', 4, 2, 'g'), ('wq2', 1), ('mm', 7), ('mm', 8), ('mm', 9), ('wint', 3, 0, 's'), ('wint', 3, 1, 's'), ('P', 6), ('Q', 6), ('P', 7), ('Q', 7), ('add', 6, 2, 'g'), ('mm', 10), ('mm', 11), ('mm', 12), ('P', 8), ('Q', 8), ('add', 8, 1, 'g'), ('mm', 13), ('P', 9), ('Q', 9), ('add', 9, 1, 'pe'), ('mm', 14), ('P', 10), ('Q', 10), ('mm', 15), ('P', 11), ('Q', 11), ('add', 10, 2, 'g'), ('wq2', 2), ('wint', 4, 0, 's'), ('wint', 4, 1, 's'), ('mm', 16), ('P', 12), ('Q', 12), ('add', 12, 1, 'g'), ('mm', 17), ('P', 13), ('Q', 13), ('add', 13, 1, 'pe'), ('mm', 18), ('P', 14), ('Q', 14), ('mm', 19), ('P', 15), ('Q', 15), ('add', 14, 2, 'g'), ('mm', 20), ('P', 16), ('Q', 16), ('add', 16, 1, 'g'), ('mm', 21), ('P', 17), ('Q', 17), ('add', 17, 1, 'pe'), ('mm', 22), ('P', 18), ('Q', 18), ('mm', 23), ('P', 19), ('Q', 19), ('add', 18, 2, 'g'), ('wq2', 3), ('wint', 5, 0, 's'), ('wint', 5, 1, 's'), ('mm', 24), ('P', 20), ('Q', 20), ('add', 20, 1, 'g'), ('mm', 25), ('P', 21), ('Q', 21), ('add', 21, 1, 'pe'), ('mm', 26), ('P', 22), ('Q', 22), ('mm', 27), ('P', 23), ('Q', 23), ('add', 22, 2, 'g'), ('mm', 28), ('P', 24), ('Q', 24), ('add', 24, 1, 'g'), ('mm', 29), ('P', 25), ('Q', 25), ('add', 25, 1, 'pe'), ('mm', 30), ('P', 26), ('Q', 26), ('mm', 31), ('P', 27), ('Q', 27), ('add', 26, 2, 'g'), ('wq2', 4), ('mm', 32), ('P', 28), ('Q', 28), ('add', 28, 1, 'g'), ('mm', 33), ('P', 29), ('Q', 29), ('add', 29, 1, 'pe'), ('mm', 34), ('P', 30), ('Q', 30), ('mm', 35), ('P', 31), ('Q', 31), ('add', 30, 2, 'g'), ('mm', 36), ('P', 32), ('Q', 32), ('add', 32, 1, 'g'), ('mm', 37), ('P', 33), ('Q', 33), ('add', 33, 1, 'pe'), ('mm', 38), ('P', 34), ('Q', 34), ('mm', 39), ('P', 35), ('Q', 35), ('add', 34, 2, 'g'), ('wq2', 5), ('mm', 40), ('P', 36), ('Q', 36), ('add', 36, 1, 'g'), ('mm', 41), ('P', 37), ('Q', 37), ('add', 37, 1, 'pe'), ('mm', 42), ('P', 38), ('Q', 38), ('mm', 43), ('P', 39), ('Q', 39), ('add', 38, 2, 'g'), ('mm', 44), ('P', 40), ('Q', 40), ('add', 40, 1, 'g'), ('mm', 45), ('P', 41), ('Q', 41), ('add', 41, 1, 'pe'), ('mm', 46), ('P', 42), ('Q', 42), ('mm', 47), ('P', 43), ('Q', 43), ('add', 42, 2, 'g'), ('P', 44), ('Q', 44), ('add', 44, 1, 'g'), ('P', 45), ('Q', 45), ('add', 45, 1, 'pe'), ('P', 46), ('Q', 46), ('P', 47), ('Q', 47), ('add', 46, 1, 'v'), ('add', 47, 1, 'v')]
+TOKENS = 1024
+K_DIM = 1024
+HEAD = 256
+HALF = HEAD // 2
+PACK = 4
+K_PASS = P * PACK
+PASSES = K_DIM // K_PASS
+TOKEN_TILES = TOKENS // P
+GROUP_HEADS = 2
+GROUP_COLS = GROUP_HEADS * HEAD
+GROUPS = 6
+TILES = GROUPS * TOKEN_TILES
+FLOPS = 2 * TOKENS * K_DIM * GROUPS * GROUP_COLS
+
+TABLE_CHUNKS = [(0, 2), (2, 4), (4, 8)]
+NEG_SIN, COS, SIN = 0, 1, 2
+
+LOOKAHEAD = 4
+TENSOR_ADD_EVERY = 4
+FIRST_TENSOR_ADD = 5
+QUANTISE_NEXT_AFTER = 3
+QUANTISE_SECOND_AFTER = 5
 
 
 def tile_gemma2attention_pa_kernel(tc, x, Wq, Wk, out_0, out_1):
@@ -37,207 +49,266 @@ def tile_gemma2attention_pa_kernel(tc, x, Wq, Wk, out_0, out_1):
         psum = ctx.enter_context(tc.psum_pool(name="psum", bufs=8))
         ctx.enter_context(tc.manual_schedule())
 
-        xr = {}
-        wr = {}
-        red = {}
-        tabs = {}
-        tabqs = {}
-        xt_ps = {}
-        xg_sb = {}
-        xc = {}
-        xs = {}
-        wg_sb = {}
-        wc = {}
-        ws = {}
-        acc_ps = {}
-        p_sb = {}
-        q_sb = {}
-        misc = {}
+        x_raw = {}
+        w_raw = {}
+        reduced = {}
+        tables = {}
+        tables_q = {}
+        x_turned = {}
+        x_grouped = {}
+        x_codes = {}
+        x_scales = {}
+        w_grouped = {}
+        w_codes = {}
+        w_scales = {}
+        sums = {}
+        first = {}
+        second = {}
 
         def load_x(t):
-            tl = keep.tile([P, D_MODEL], BF16, name="xr%d" % t)
-            nc.sync.dma_start(out=tl[:], in_=x[0, t * P:(t + 1) * P, :])
-            xr[t] = tl
+            x_raw[t] = keep.tile([P, K_DIM], BF16, name="x_raw%d" % t)
+            nc.sync.dma_start(out=x_raw[t][:], in_=x[0, t * P:(t + 1) * P, :])
 
         def load_w(g, c):
-            src = groups[g][0]
-            h0 = groups[g][2]
-            tl = keep.tile([P, 2, 4, H], BF16, name="wr%d_%d" % (g, c))
+            weights, h0 = groups[g][0], groups[g][2]
+            w_raw[(g, c)] = keep.tile([P, GROUP_HEADS, PACK, HEAD], BF16, name="w_raw%d_%d" % (g, c))
             nc.sync.dma_start(
-                out=tl[:],
-                in_=src[h0:h0 + 2, c * 512:(c + 1) * 512, :].rearrange("h (p j) w -> p h j w", j=4))
-            wr[(g, c)] = tl
+                out=w_raw[(g, c)][:],
+                in_=weights[h0:h0 + GROUP_HEADS, c * K_PASS:(c + 1) * K_PASS, :].rearrange(
+                    "h (p j) w -> p h j w", j=PACK))
 
-        def const():
-            ang = keep.tile([P, NT, HALF], F32, name="ang")
-            nc.gpsimd.iota(ang[:, :, 0], pattern=[[P, NT]], base=0, channel_multiplier=1,
+        angle = keep.tile([P, TOKEN_TILES, HALF], F32, name="angle")
+        identity = keep.tile([P, P], F32, name="identity")
+        warm = keep.tile([P, 2], F32, name="warm")
+
+        def make_angles():
+            nc.gpsimd.iota(angle[:, :, 0], pattern=[[P, TOKEN_TILES]], base=0, channel_multiplier=1,
                            allow_small_or_imprecise_dtypes=True)
-            ident = keep.tile([P, P], F32, name="ident")
-            make_identity(nc, ident[:])
-            junk = keep.tile([P, 2], F32, name="junk")
-            nc.vector.memset(junk[:, 0:1], 0.0)
-            nc.scalar.activation(out=junk[:, 1:2], in_=junk[:, 0:1], func=ACT.Sin)
+            make_identity(nc, identity[:])
+            nc.vector.memset(warm[:, 0:1], 0.0)
+            nc.scalar.activation(out=warm[:, 1:2], in_=warm[:, 0:1], func=ACT.Sin)
             ratio = 10000.0 ** (-1.0 / HALF)
             k = 1
             while k < HALF:
-                nc.vector.tensor_scalar(out=ang[:, :, k:2 * k], in0=ang[:, :, 0:k], scalar1=ratio ** k,
+                nc.vector.tensor_scalar(out=angle[:, :, k:2 * k], in0=angle[:, :, 0:k], scalar1=ratio ** k,
                                         scalar2=None, op0=ALU.mult)
                 k *= 2
-            misc["ang"] = ang
-            misc["ident"] = ident
 
-        def reduce_angle(key, n):
-            t0 = 0 if key == 0 else 2
-            a = misc["ang"][:, t0:t0 + n, :]
-            ti = keep.tile([P, n, HALF], I32, name="ti%d" % key)
-            nc.vector.tensor_scalar(out=ti[:], in0=a, scalar1=1.0 / (2.0 * math.pi),
-                                    scalar2=None, op0=ALU.mult)
-            tf = keep.tile([P, n, HALF], F32, name="tf%d" % key)
-            nc.vector.tensor_copy(out=tf[:], in_=ti[:])
-            r = keep.tile([P, n, HALF], F32, name="red%d" % key)
-            nc.vector.scalar_tensor_tensor(out=r[:].rearrange("p t i -> p (t i)"),
-                                           in0=tf[:].rearrange("p t i -> p (t i)"),
+        def reduce_angles(key, t0, t1):
+            part = angle[:, t0:t1, :]
+            turns = keep.tile([P, t1 - t0, HALF], I32, name="turns%d" % key)
+            nc.vector.tensor_scalar(out=turns[:], in0=part, scalar1=1.0 / (2.0 * math.pi), scalar2=None,
+                                    op0=ALU.mult)
+            reduced[key] = keep.tile([P, t1 - t0, HALF], F32, name="reduced%d" % key)
+            nc.vector.scalar_tensor_tensor(out=reduced[key][:].rearrange("p t i -> p (t i)"),
+                                           in0=turns[:].rearrange("p t i -> p (t i)"),
                                            scalar=-2.0 * math.pi,
-                                           in1=a.rearrange("p t i -> p (t i)"),
+                                           in1=part.rearrange("p t i -> p (t i)"),
                                            op0=ALU.mult, op1=ALU.add)
-            red[key] = r
 
-        def trig(ci, key, n):
-            off = 2 if ci == 2 else 0
-            r = red[key][:, off:off + n, :]
-            tb = keep.tile([P, 3, n, HALF], F32, name="tab%d" % ci)
-            ab = keep.tile([P, n, HALF], F32, name="abs%d" % ci)
-            nc.scalar.activation(out=tb[:, 2, :, :], in_=r, func=ACT.Sin)
-            nc.scalar.activation(out=ab[:], in_=r, func=ACT.Abs)
-            nc.scalar.activation(out=tb[:, 1, :, :], in_=ab[:], func=ACT.Sin, scale=-1.0, bias=math.pi / 2.0)
-            nc.gpsimd.tensor_scalar(out=tb[:, 0, :, :], in0=tb[:, 2, :, :], scalar1=-1.0, scalar2=0.0,
-                                    op0=ALU.mult, op1=ALU.add)
-            tabs[ci] = tb
+        def make_table(chunk, key, offset):
+            count = TABLE_CHUNKS[chunk][1] - TABLE_CHUNKS[chunk][0]
+            part = reduced[key][:, offset:offset + count, :]
+            tables[chunk] = keep.tile([P, 3, count, HALF], F32, name="table%d" % chunk)
+            magnitude = keep.tile([P, count, HALF], F32, name="magnitude%d" % chunk)
+            nc.scalar.activation(out=tables[chunk][:, SIN, :, :], in_=part, func=ACT.Sin)
+            nc.scalar.activation(out=magnitude[:], in_=part, func=ACT.Abs)
+            nc.scalar.activation(out=tables[chunk][:, COS, :, :], in_=magnitude[:], func=ACT.Sin,
+                                 scale=-1.0, bias=math.pi / 2.0)
+            nc.gpsimd.tensor_scalar(out=tables[chunk][:, NEG_SIN, :, :], in0=tables[chunk][:, SIN, :, :],
+                                    scalar1=-1.0, scalar2=0.0, op0=ALU.mult, op1=ALU.add)
 
-        def scale_tables():
-            for ci in range(len(CHUNKS)):
-                t0, t1 = CHUNKS[ci]
-                tq = keep.tile([P, 3, t1 - t0, HALF], F32, name="tabq%d" % ci)
-                nc.scalar.activation(out=tq[:], in_=tabs[ci][:], func=ACT.Copy, scale=1.0 / 16.0)
-                tabqs[ci] = tq
+        def make_tables_q():
+            for chunk in range(len(TABLE_CHUNKS)):
+                count = TABLE_CHUNKS[chunk][1] - TABLE_CHUNKS[chunk][0]
+                tables_q[chunk] = keep.tile([P, 3, count, HALF], F32, name="table_q%d" % chunk)
+                nc.scalar.activation(out=tables_q[chunk][:], in_=tables[chunk][:], func=ACT.Copy, scale=1.0 / 16.0)
 
-        def table_of(t, scaled):
-            for ci in range(len(CHUNKS)):
-                t0, t1 = CHUNKS[ci]
+        def table_of(t, divided):
+            for chunk in range(len(TABLE_CHUNKS)):
+                t0, t1 = TABLE_CHUNKS[chunk]
                 if t0 <= t < t1:
-                    return (tabqs[ci] if scaled else tabs[ci]), t - t0
-            return None, 0
+                    return (tables_q[chunk] if divided else tables[chunk]), t - t0
+            raise ValueError("no table for token tile %d" % t)
 
-        def x_transpose(t):
-            words = xr[t][:].bitcast(F32)
-            xt = psum.tile([P, NPASS, 2, P], F32, tag="bank", name="xt")
-            for c in range(NPASS):
+        def turn_x(t):
+            words = x_raw[t][:].bitcast(F32)
+            x_turned[t] = psum.tile([P, PASSES, 2, P], F32, tag="bank", name="x_turned")
+            for c in range(PASSES):
                 for u in range(2):
-                    nc.tensor.transpose(xt[:, c, u, :], words[:, 256 * c + u:256 * (c + 1):2], misc["ident"][:])
-            xt_ps[t] = xt
+                    nc.tensor.transpose(x_turned[t][:, c, u, :], words[:, 256 * c + u:256 * (c + 1):2],
+                                        identity[:])
 
-        def x_evac(t):
-            if t % 2 == 0:
-                xg_new = stage.tile([P, 2, 1024], BF16, tag="xg", bufs=4, name="xg", align_bytes=64)
-                xg_sb[t // 2] = xg_new
-                xc_new = keep.tile([P, 2, 256], U32, name="xc%d" % (t // 2), align_bytes=64)
-                xs_new = keep.tile([P, 2, 256], U8, name="xs%d" % (t // 2), align_bytes=64)
-                xc[t // 2] = xc_new
-                xs[t // 2] = xs_new
-            nc.scalar.copy(out=xg_sb[t // 2][:, t % 2, :].bitcast(F32).rearrange("p (c r u) -> p c r u", c=NPASS, u=2),
-                           in_=xt_ps[t][:].rearrange("p c u r -> p c r u"))
+        def group_x(t):
+            pair, slot = divmod(t, 2)
+            if slot == 0:
+                x_grouped[pair] = stage.tile([P, 2, PASSES * P * PACK], BF16, tag="x_grouped", bufs=4,
+                                             name="x_grouped", align_bytes=64)
+                x_codes[pair] = keep.tile([P, 2, PASSES * P], U32, name="x_codes%d" % pair, align_bytes=64)
+                x_scales[pair] = keep.tile([P, 2, PASSES * P], U8, name="x_scales%d" % pair, align_bytes=64)
+            nc.scalar.copy(
+                out=x_grouped[pair][:, slot, :].bitcast(F32).rearrange("p (c r u) -> p c r u", c=PASSES, u=2),
+                in_=x_turned[t][:].rearrange("p c u r -> p c r u"))
 
-        def x_quant(t):
-            nc.vector.quantize_mx(out=xc[t // 2][:, t % 2, :].bitcast(FP8X4), scales=xs[t // 2][:, t % 2, :],
-                                  in_=xg_sb[t // 2][:, t % 2, :])
+        def bring_x(t):
+            turn_x(t)
+            group_x(t)
 
-        def x_quant2(t):
-            nc.vector.quantize_mx(out=xc[t // 2][:].rearrange("p a n -> p (a n)").bitcast(FP8X4),
-                                  scales=xs[t // 2][:].rearrange("p a n -> p (a n)"),
-                                  in_=xg_sb[t // 2][:].rearrange("p a n -> p (a n)"))
+        def quantise_x(t):
+            pair, slot = divmod(t, 2)
+            nc.vector.quantize_mx(out=x_codes[pair][:, slot, :].bitcast(FP8X4), scales=x_scales[pair][:, slot, :],
+                                  in_=x_grouped[pair][:, slot, :])
 
-        def w_inter(g, c, eng):
+        def quantise_x_pair(pair):
+            nc.vector.quantize_mx(out=x_codes[pair][:].rearrange("p a n -> p (a n)").bitcast(FP8X4),
+                                  scales=x_scales[pair][:].rearrange("p a n -> p (a n)"),
+                                  in_=x_grouped[pair][:].rearrange("p a n -> p (a n)"))
+
+        def group_w(g, c, engine):
             if c == 0:
-                wg_new = stage.tile([P, 2, 2048], BF16, tag="wg", bufs=3, name="wg", align_bytes=64)
-                wg_sb[g] = wg_new
-                wc_new = keep.tile([P, 2, 512], U32, name="wc%d" % g, align_bytes=64)
-                ws_new = keep.tile([P, 2, 512], U8, name="ws%d" % g, align_bytes=64)
-                wc[g] = wc_new
-                ws[g] = ws_new
-            dst = wg_sb[g][:, c, :].rearrange("p (h w j) -> p h w j", h=2, j=4)
-            src = wr[(g, c)][:].rearrange("p h j w -> p h w j")
-            if eng == "v":
-                nc.vector.tensor_copy(out=dst, in_=src)
+                w_grouped[g] = stage.tile([P, PASSES, GROUP_COLS * PACK], BF16, tag="w_grouped", bufs=3,
+                                          name="w_grouped", align_bytes=64)
+                w_codes[g] = keep.tile([P, PASSES, GROUP_COLS], U32, name="w_codes%d" % g, align_bytes=64)
+                w_scales[g] = keep.tile([P, PASSES, GROUP_COLS], U8, name="w_scales%d" % g, align_bytes=64)
+            target = w_grouped[g][:, c, :].rearrange("p (h w j) -> p h w j", h=GROUP_HEADS, j=PACK)
+            source = w_raw[(g, c)][:].rearrange("p h j w -> p h w j")
+            if engine == "vector":
+                nc.vector.tensor_copy(out=target, in_=source)
             else:
-                nc.scalar.copy(out=dst, in_=src)
+                nc.scalar.copy(out=target, in_=source)
 
-        def w_quant(g, c):
-            nc.vector.quantize_mx(out=wc[g][:, c, :].bitcast(FP8X4), scales=ws[g][:, c, :], in_=wg_sb[g][:, c, :])
+        def quantise_w_pass(g, c):
+            nc.vector.quantize_mx(out=w_codes[g][:, c, :].bitcast(FP8X4), scales=w_scales[g][:, c, :],
+                                  in_=w_grouped[g][:, c, :])
 
-        def w_quant2(g):
-            nc.vector.quantize_mx(out=wc[g][:].rearrange("p a n -> p (a n)").bitcast(FP8X4),
-                                  scales=ws[g][:].rearrange("p a n -> p (a n)"),
-                                  in_=wg_sb[g][:].rearrange("p a n -> p (a n)"))
+        def quantise_w(g):
+            nc.vector.quantize_mx(out=w_codes[g][:].rearrange("p c n -> p (c n)").bitcast(FP8X4),
+                                  scales=w_scales[g][:].rearrange("p c n -> p (c n)"),
+                                  in_=w_grouped[g][:].rearrange("p c n -> p (c n)"))
 
-        def mm(n):
-            g, t = divmod(n, NT)
-            acc = psum.tile([P, 512], F32, tag="bank", name="acc")
-            for c in range(NPASS):
-                nc.tensor.matmul_mx(out=acc[:],
-                                    lhsT=xc[t // 2][:, t % 2, c * P:(c + 1) * P].bitcast(FP8X4),
-                                    lhsT_scale=xs[t // 2][:, t % 2, c * P:(c + 1) * P],
-                                    rhs=wc[g][:, c, :].bitcast(FP8X4),
-                                    rhs_scale=ws[g][:, c, :],
-                                    start=(c == 0), stop=(c == NPASS - 1))
-            acc_ps[n] = acc
+        def project(n):
+            g, t = divmod(n, TOKEN_TILES)
+            pair, slot = divmod(t, 2)
+            sums[n] = psum.tile([P, GROUP_COLS], F32, tag="bank", name="sums")
+            for c in range(PASSES):
+                nc.tensor.matmul_mx(out=sums[n][:],
+                                    lhsT=x_codes[pair][:, slot, c * P:(c + 1) * P].bitcast(FP8X4),
+                                    lhsT_scale=x_scales[pair][:, slot, c * P:(c + 1) * P],
+                                    rhs=w_codes[g][:, c, :].bitcast(FP8X4),
+                                    rhs_scale=w_scales[g][:, c, :],
+                                    start=(c == 0), stop=(c == PASSES - 1))
 
-        def rope_half(n, f):
-            g, t = divmod(n, NT)
-            table, tl = table_of(t, groups[g][3])
-            accv = acc_ps[n][:].rearrange("p (h f i) -> p h f i", h=2, f=2)
-            shape = [P, 2, HALF, 2]
-            a = n % 2
-            if a == 0 and f == 0:
-                pt_new = stage.tile([P, 2, 512], F32, tag="pt", bufs=4, name="pt")
-                qt_new = stage.tile([P, 2, 512], F32, tag="qt", bufs=3, name="qt")
-                p_sb[n // 2] = pt_new
-                q_sb[n // 2] = qt_new
-            dst = p_sb[n // 2] if f == 0 else q_sb[n // 2]
-            nc.vector.tensor_tensor(
-                out=dst[:, a, :].rearrange("p (h i e) -> p h i e", h=2, e=2),
-                in0=accv[:, :, f, :].unsqueeze(3).to_broadcast(shape),
-                in1=table[:, 1 - f:3 - f, tl, :].rearrange("p e i -> p i e").unsqueeze(1).to_broadcast(shape),
-                op=ALU.mult)
+        def rotate(n):
+            g, t = divmod(n, TOKEN_TILES)
+            table, row = table_of(t, groups[g][3])
+            pair, slot = divmod(n, 2)
+            if slot == 0:
+                first[pair] = stage.tile([P, 2, GROUP_COLS], F32, tag="first", bufs=4, name="first")
+                second[pair] = stage.tile([P, 2, GROUP_COLS], F32, tag="second", bufs=3, name="second")
+            halves = sums[n][:].rearrange("p (h f i) -> p h f i", h=GROUP_HEADS, f=2)
+            shape = [P, GROUP_HEADS, HALF, 2]
+            for f, product, plane in ((0, first[pair], COS), (1, second[pair], NEG_SIN)):
+                nc.vector.tensor_tensor(
+                    out=product[:, slot, :].rearrange("p (h i e) -> p h i e", h=GROUP_HEADS, e=2),
+                    in0=halves[:, :, f, :].unsqueeze(3).to_broadcast(shape),
+                    in1=table[:, plane:plane + 2, row, :].rearrange("p e i -> p i e").unsqueeze(1).to_broadcast(shape),
+                    op=ALU.mult)
 
-        def rope_p(n):
-            rope_half(n, 0)
-
-        def rope_q(n):
-            rope_half(n, 1)
-
-        def add_store(n, count, eng):
-            g, t = divmod(n, NT)
-            dst = groups[g][1]
-            h0 = groups[g][2]
-            a = n % 2
-            pt = p_sb[n // 2][:, a:a + count, :]
-            qt = q_sb[n // 2][:, a:a + count, :]
-            if eng == "v":
-                nc.vector.tensor_tensor(out=pt, in0=pt, in1=qt, op=ALU.add)
-            elif eng == "pe":
-                bank = psum.tile([P, 512], F32, tag="bank", name="sumbank")
-                nc.tensor.matmul(out=bank[:], lhsT=misc["ident"][:], rhs=p_sb[n // 2][:, a, :], start=True, stop=False)
-                nc.tensor.matmul(out=bank[:], lhsT=misc["ident"][:], rhs=q_sb[n // 2][:, a, :], start=False, stop=True)
-                nc.scalar.copy(out=p_sb[n // 2][:, a, :], in_=bank[:])
+        def add_and_store(n, count, engine):
+            g, t = divmod(n, TOKEN_TILES)
+            target, h0 = groups[g][1], groups[g][2]
+            pair, slot = divmod(n, 2)
+            a = first[pair][:, slot:slot + count, :]
+            b = second[pair][:, slot:slot + count, :]
+            if engine == "vector":
+                nc.vector.tensor_tensor(out=a, in0=a, in1=b, op=ALU.add)
+            elif engine == "gpsimd":
+                nc.gpsimd.tensor_tensor(out=a, in0=a, in1=b, op=ALU.add)
             else:
-                nc.gpsimd.tensor_tensor(out=pt, in0=pt, in1=qt, op=ALU.add)
+                total = psum.tile([P, GROUP_COLS], F32, tag="bank", name="total")
+                nc.tensor.matmul(out=total[:], lhsT=identity[:], rhs=first[pair][:, slot, :], start=True, stop=False)
+                nc.tensor.matmul(out=total[:], lhsT=identity[:], rhs=second[pair][:, slot, :], start=False, stop=True)
+                nc.scalar.copy(out=first[pair][:, slot, :], in_=total[:])
             nc.sync.dma_start(
-                out=dst[0, t * P:(t + count) * P, h0:h0 + 2, :].rearrange("(a p) h d -> p a h d", p=P),
-                in_=pt.rearrange("p a (h d) -> p a h d", h=2))
+                out=target[0, t * P:(t + count) * P, h0:h0 + GROUP_HEADS, :].rearrange("(a p) h d -> p a h d", p=P),
+                in_=a.rearrange("p a (h d) -> p a h d", h=GROUP_HEADS))
 
-        stages = {"loadw": load_w, "loadx": load_x, "const": const, "red": reduce_angle, "trig": trig,
-                  "tabq": scale_tables, "xT": x_transpose, "xev": x_evac, "xq": x_quant, "xq2": x_quant2,
-                  "wint": w_inter, "wq": w_quant, "wq2": w_quant2, "mm": mm, "P": rope_p, "Q": rope_q,
-                  "add": add_store}
-        for step in SCHEDULE:
-            stages[step[0]](*step[1:])
+        load_w(0, 0)
+        load_x(0)
+        load_w(0, 1)
+        for t in range(1, TOKEN_TILES):
+            load_x(t)
+        for g in range(1, GROUPS):
+            for c in range(PASSES):
+                load_w(g, c)
+
+        make_angles()
+        reduce_angles(0, 0, 2)
+        make_table(0, 0, 0)
+        reduce_angles(1, 2, 8)
+        group_w(0, 0, "vector")
+        bring_x(0)
+        group_w(0, 1, "scalar")
+        bring_x(1)
+        make_table(1, 1, 0)
+        bring_x(2)
+        quantise_w_pass(0, 0)
+        quantise_x(0)
+        quantise_w_pass(0, 1)
+        quantise_x(1)
+        for t in (3, 4, 5):
+            bring_x(t)
+        project(0)
+        project(1)
+        make_table(2, 1, 2)
+        for t in (6, 7):
+            bring_x(t)
+        for g in (1, 2):
+            for c in range(PASSES):
+                group_w(g, c, "scalar")
+        make_tables_q()
+
+        projected = [2]
+        x_ready = [2]
+        groups_ready = [1]
+
+        def project_up_to(limit):
+            while projected[0] < min(limit, TILES, groups_ready[0] * TOKEN_TILES):
+                if projected[0] < TOKEN_TILES and projected[0] >= x_ready[0]:
+                    break
+                project(projected[0])
+                projected[0] += 1
+
+        for n in range(TILES):
+            g, t = divmod(n, TOKEN_TILES)
+            project_up_to(n + LOOKAHEAD + 1 if g > 0 else n + 2)
+            rotate(n)
+
+            phase = n % TENSOR_ADD_EVERY
+            if n == TILES - 1:
+                add_and_store(n - 1, 1, "vector")
+                add_and_store(n, 1, "vector")
+            elif n == TILES - 2:
+                pass
+            elif n < FIRST_TENSOR_ADD - 1:
+                if n % 2 == 1:
+                    add_and_store(n - 1, 2, "gpsimd")
+            elif phase == 0:
+                add_and_store(n, 1, "gpsimd")
+            elif phase == 1:
+                add_and_store(n, 1, "tensor")
+            elif phase == 3:
+                add_and_store(n - 1, 2, "gpsimd")
+
+            if g == 0 and t in (0, 1, 3):
+                pair = (1, 2, 0, 3)[t]
+                quantise_x_pair(pair)
+                x_ready[0] = 2 * pair + 2
+                project_up_to(n + 3)
+            if g + 1 < GROUPS and t == (QUANTISE_SECOND_AFTER if g == 0 else QUANTISE_NEXT_AFTER):
+                quantise_w(g + 1)
+                groups_ready[0] = g + 2
+                if g + 3 < GROUPS:
+                    for c in range(PASSES):
+                        group_w(g + 3, c, "scalar")
+                project_up_to(n + LOOKAHEAD + 1)

@@ -170,12 +170,14 @@ def tile_gemma2attention_pa_kernel(tc, x, Wq, Wk, out_0, out_1):
                                           name="w_grouped", align_bytes=64)
                 w_codes[g] = keep.tile([P, PASSES, GROUP_COLS], U32, name="w_codes%d" % g, align_bytes=64)
                 w_scales[g] = keep.tile([P, PASSES, GROUP_COLS], U8, name="w_scales%d" % g, align_bytes=64)
-            target = w_grouped[g][:, c, :].rearrange("p (h w j) -> p h w j", h=GROUP_HEADS, j=PACK)
-            source = w_raw[(g, c)][:].rearrange("p h j w -> p h w j")
-            if engine == "vector":
-                nc.vector.tensor_copy(out=target, in_=source)
-            else:
-                nc.scalar.copy(out=target, in_=source)
+            for h in range(GROUP_HEADS):
+                target = w_grouped[g][:, c, h * HEAD * PACK:(h + 1) * HEAD * PACK].rearrange(
+                    "p (q i j) -> p q j i", i=4, j=PACK)
+                source = w_raw[(g, c)][:, h, :, :].rearrange("p j (q i) -> p q j i", i=4)
+                if engine == "vector":
+                    nc.vector.tensor_copy(out=target, in_=source)
+                else:
+                    nc.scalar.copy(out=target, in_=source)
 
         def quantise_w_pass(g, c):
             nc.vector.quantize_mx(out=w_codes[g][:, c, :].bitcast(FP8X4), scales=w_scales[g][:, c, :],

@@ -29,7 +29,6 @@ TILES = GROUPS * TOKEN_TILES
 FLOPS = 2 * TOKENS * K_DIM * GROUPS * GROUP_COLS
 
 TABLE_CHUNKS = [(0, 2), (2, 4), (4, 8)]
-NEG_SIN, COS, SIN = 0, 1, 2
 
 LOOKAHEAD = 4
 TENSOR_ADD_EVERY = 4
@@ -62,8 +61,8 @@ def tile_gemma2attention_pa_kernel(tc, x, Wq, Wk, out_0, out_1):
         w_codes = {}
         w_scales = {}
         sums = {}
-        first = {}
-        second = {}
+        products = {}
+        result = {}
 
         def load_x(t):
             x_raw[t] = keep.tile([P, K_DIM], BF16, name="x_raw%d" % t)
@@ -109,20 +108,23 @@ def tile_gemma2attention_pa_kernel(tc, x, Wq, Wk, out_0, out_1):
         def make_table(chunk, key, offset):
             count = TABLE_CHUNKS[chunk][1] - TABLE_CHUNKS[chunk][0]
             part = reduced[key][:, offset:offset + count, :]
-            tables[chunk] = keep.tile([P, 3, count, HALF], F32, name="table%d" % chunk)
+            tables[chunk] = keep.tile([P, 2, count, 2, HALF], F32, name="table%d" % chunk)
             magnitude = keep.tile([P, count, HALF], F32, name="magnitude%d" % chunk)
-            nc.scalar.activation(out=tables[chunk][:, SIN, :, :], in_=part, func=ACT.Sin)
+            nc.scalar.activation(out=tables[chunk][:, 1, :, 0, :], in_=part, func=ACT.Sin)
             nc.scalar.activation(out=magnitude[:], in_=part, func=ACT.Abs)
-            nc.scalar.activation(out=tables[chunk][:, COS, :, :], in_=magnitude[:], func=ACT.Sin,
+            nc.scalar.activation(out=tables[chunk][:, 0, :, 0, :], in_=magnitude[:], func=ACT.Sin,
                                  scale=-1.0, bias=math.pi / 2.0)
-            nc.gpsimd.tensor_scalar(out=tables[chunk][:, NEG_SIN, :, :], in0=tables[chunk][:, SIN, :, :],
+            nc.gpsimd.tensor_scalar(out=tables[chunk][:, 0, :, 1, :], in0=tables[chunk][:, 1, :, 0, :],
                                     scalar1=-1.0, scalar2=0.0, op0=ALU.mult, op1=ALU.add)
+            nc.gpsimd.tensor_scalar(out=tables[chunk][:, 1, :, 1, :], in0=tables[chunk][:, 0, :, 0, :],
+                                    scalar1=1.0, scalar2=0.0, op0=ALU.mult, op1=ALU.add)
 
         def make_tables_q():
             for chunk in range(len(TABLE_CHUNKS)):
                 count = TABLE_CHUNKS[chunk][1] - TABLE_CHUNKS[chunk][0]
-                tables_q[chunk] = keep.tile([P, 3, count, HALF], F32, name="table_q%d" % chunk)
-                nc.scalar.activation(out=tables_q[chunk][:], in_=tables[chunk][:], func=ACT.Copy, scale=1.0 / 16.0)
+                tables_q[chunk] = keep.tile([P, 2, count, 2, HALF], F32, name="table_q%d" % chunk)
+                nc.scalar.activation(out=tables_q[chunk][:].rearrange("p e t f i -> p (e t f i)"),
+                                     in_=tables[chunk][:].rearrange("p e t f i -> p (e t f i)"), func=ACT.Copy, scale=1.0 / 16.0)
 
         def table_of(t, divided):
             for chunk in range(len(TABLE_CHUNKS)):
@@ -205,35 +207,34 @@ def tile_gemma2attention_pa_kernel(tc, x, Wq, Wk, out_0, out_1):
             table, row = table_of(t, groups[g][3])
             pair, slot = divmod(n, 2)
             if slot == 0:
-                first[pair] = stage.tile([P, 2, GROUP_COLS], F32, tag="first", bufs=4, name="first")
-                second[pair] = stage.tile([P, 2, GROUP_COLS], F32, tag="second", bufs=3, name="second")
-            halves = sums[n][:].rearrange("p (h f i) -> p h f i", h=GROUP_HEADS, f=2)
-            shape = [P, GROUP_HEADS, HALF, 2]
-            for f, product, plane in ((0, first[pair], COS), (1, second[pair], NEG_SIN)):
-                nc.vector.tensor_tensor(
-                    out=product[:, slot, :].rearrange("p (h i e) -> p h i e", h=GROUP_HEADS, e=2),
-                    in0=halves[:, :, f, :].unsqueeze(3).to_broadcast(shape),
-                    in1=table[:, plane:plane + 2, row, :].rearrange("p e i -> p i e").unsqueeze(1).to_broadcast(shape),
-                    op=ALU.mult)
+                products[pair] = stage.tile([P, 2, GROUP_HEADS, 2, HEAD], F32, tag="products", bufs=3, name="products")
+                result[pair] = stage.tile([P, 2, GROUP_COLS], F32, tag="result", bufs=4, name="result")
+            shape = [P, GROUP_HEADS, HEAD, 2]
+            nc.vector.tensor_tensor(
+                out=products[pair][:, slot, :, :, :].rearrange("p h f (i e) -> p h (f i) e", e=2),
+                in0=sums[n][:].rearrange("p (h m) -> p h m", h=GROUP_HEADS).unsqueeze(3).to_broadcast(shape),
+                in1=table[:, :, row, :, :].rearrange("p e f i -> p (f i) e").unsqueeze(1).to_broadcast(shape),
+                op=ALU.mult)
 
         def add_and_store(n, count, engine):
             g, t = divmod(n, TOKEN_TILES)
             target, h0 = groups[g][1], groups[g][2]
             pair, slot = divmod(n, 2)
-            a = first[pair][:, slot:slot + count, :]
-            b = second[pair][:, slot:slot + count, :]
+            a = products[pair][:, slot:slot + count, :, 0, :]
+            b = products[pair][:, slot:slot + count, :, 1, :]
+            r = result[pair][:, slot:slot + count, :].rearrange("p a (h d) -> p a h d", h=GROUP_HEADS)
             if engine == "vector":
-                nc.vector.tensor_tensor(out=a, in0=a, in1=b, op=ALU.add)
+                nc.vector.tensor_tensor(out=r, in0=a, in1=b, op=ALU.add)
             elif engine == "gpsimd":
-                nc.gpsimd.tensor_tensor(out=a, in0=a, in1=b, op=ALU.add)
+                nc.gpsimd.tensor_tensor(out=r, in0=a, in1=b, op=ALU.add)
             else:
-                total = psum.tile([P, GROUP_COLS], F32, tag="bank", name="total")
-                nc.tensor.matmul(out=total[:], lhsT=identity[:], rhs=first[pair][:, slot, :], start=True, stop=False)
-                nc.tensor.matmul(out=total[:], lhsT=identity[:], rhs=second[pair][:, slot, :], start=False, stop=True)
-                nc.scalar.copy(out=first[pair][:, slot, :], in_=total[:])
+                total = psum.tile([P, GROUP_HEADS, HEAD], F32, tag="bank", name="total")
+                nc.tensor.matmul(out=total[:], lhsT=identity[:], rhs=products[pair][:, slot, :, 0, :], start=True, stop=False)
+                nc.tensor.matmul(out=total[:], lhsT=identity[:], rhs=products[pair][:, slot, :, 1, :], start=False, stop=True)
+                nc.scalar.copy(out=result[pair][:, slot, :], in_=total[:].rearrange("p h d -> p (h d)"))
             nc.sync.dma_start(
                 out=target[0, t * P:(t + count) * P, h0:h0 + GROUP_HEADS, :].rearrange("(a p) h d -> p a h d", p=P),
-                in_=a.rearrange("p a (h d) -> p a h d", h=GROUP_HEADS))
+                in_=r)
 
         load_w(0, 0)
         load_x(0)

@@ -34,7 +34,7 @@ LOOKAHEAD = 4
 TENSOR_ADD_EVERY = 4
 FIRST_TENSOR_ADD = 5
 QUANTISE_NEXT_AFTER = 3
-QUANTISE_SECOND_AFTER = 5
+QUANTISE_SECOND_AFTER = 6
 
 
 def tile_gemma2attention_pa_kernel(tc, x, Wq, Wk, out_0, out_1):
@@ -50,6 +50,7 @@ def tile_gemma2attention_pa_kernel(tc, x, Wq, Wk, out_0, out_1):
 
         x_raw = {}
         w_raw = {}
+        turns = {}
         reduced = {}
         tables = {}
         tables_q = {}
@@ -93,14 +94,16 @@ def tile_gemma2attention_pa_kernel(tc, x, Wq, Wk, out_0, out_1):
                                         scalar2=None, op0=ALU.mult)
                 k *= 2
 
+        def count_turns(key, t0, t1):
+            turns[key] = keep.tile([P, t1 - t0, HALF], I32, name="turns%d" % key)
+            nc.vector.tensor_scalar(out=turns[key][:], in0=angle[:, t0:t1, :], scalar1=1.0 / (2.0 * math.pi),
+                                    scalar2=None, op0=ALU.mult)
+
         def reduce_angles(key, t0, t1):
             part = angle[:, t0:t1, :]
-            turns = keep.tile([P, t1 - t0, HALF], I32, name="turns%d" % key)
-            nc.vector.tensor_scalar(out=turns[:], in0=part, scalar1=1.0 / (2.0 * math.pi), scalar2=None,
-                                    op0=ALU.mult)
             reduced[key] = keep.tile([P, t1 - t0, HALF], F32, name="reduced%d" % key)
             nc.vector.scalar_tensor_tensor(out=reduced[key][:].rearrange("p t i -> p (t i)"),
-                                           in0=turns[:].rearrange("p t i -> p (t i)"),
+                                           in0=turns[key][:].rearrange("p t i -> p (t i)"),
                                            scalar=-2.0 * math.pi,
                                            in1=part.rearrange("p t i -> p (t i)"),
                                            op0=ALU.mult, op1=ALU.add)
@@ -166,13 +169,13 @@ def tile_gemma2attention_pa_kernel(tc, x, Wq, Wk, out_0, out_1):
                                   scales=x_scales[pair][:].rearrange("p a n -> p (a n)"),
                                   in_=x_grouped[pair][:].rearrange("p a n -> p (a n)"))
 
-        def group_w(g, c, engine):
-            if c == 0:
+        def group_w(g, c, engine, heads=(0, 1)):
+            if g not in w_grouped:
                 w_grouped[g] = stage.tile([P, PASSES, GROUP_COLS * PACK], BF16, tag="w_grouped", bufs=3,
                                           name="w_grouped", align_bytes=64)
                 w_codes[g] = keep.tile([P, PASSES, GROUP_COLS], U32, name="w_codes%d" % g, align_bytes=64)
                 w_scales[g] = keep.tile([P, PASSES, GROUP_COLS], U8, name="w_scales%d" % g, align_bytes=64)
-            for h in range(GROUP_HEADS):
+            for h in heads:
                 target = w_grouped[g][:, c, h * HEAD * PACK:(h + 1) * HEAD * PACK].rearrange(
                     "p (q i j) -> p q j i", i=4, j=PACK)
                 source = w_raw[(g, c)][:, h, :, :].rearrange("p j (q i) -> p q j i", i=4)
@@ -246,29 +249,31 @@ def tile_gemma2attention_pa_kernel(tc, x, Wq, Wk, out_0, out_1):
                 load_w(g, c)
 
         make_angles()
+        group_w(0, 0, "vector", heads=(0,))
+        count_turns(0, 0, 2)
+        group_w(0, 0, "vector", heads=(1,))
         reduce_angles(0, 0, 2)
-        make_table(0, 0, 0)
-        reduce_angles(1, 2, 8)
-        group_w(0, 0, "vector")
         bring_x(0)
-        group_w(0, 1, "scalar")
-        bring_x(1)
-        make_table(1, 1, 0)
-        bring_x(2)
+        make_table(0, 0, 0)
+        group_w(0, 1, "vector")
+        for t in (1, 2, 3, 4, 5):
+            bring_x(t)
         quantise_w_pass(0, 0)
         quantise_x(0)
         quantise_w_pass(0, 1)
-        quantise_x(1)
-        for t in (3, 4, 5):
-            bring_x(t)
         project(0)
+        count_turns(1, 2, 8)
+        quantise_x(1)
+        reduce_angles(1, 2, 8)
         project(1)
+        make_table(1, 1, 0)
         make_table(2, 1, 2)
         for t in (6, 7):
             bring_x(t)
-        for g in (1, 2):
-            for c in range(PASSES):
-                group_w(g, c, "scalar")
+        group_w(1, 0, "scalar", heads=(1,))
+        group_w(1, 1, "scalar")
+        for c in range(PASSES):
+            group_w(2, c, "scalar")
         make_tables_q()
 
         projected = [2]
@@ -308,6 +313,8 @@ def tile_gemma2attention_pa_kernel(tc, x, Wq, Wk, out_0, out_1):
                 quantise_x_pair(pair)
                 x_ready[0] = 2 * pair + 2
                 project_up_to(n + 3)
+            if n == 1:
+                group_w(1, 0, "vector", heads=(0,))
             if g + 1 < GROUPS and t == (QUANTISE_SECOND_AFTER if g == 0 else QUANTISE_NEXT_AFTER):
                 quantise_w(g + 1)
                 groups_ready[0] = g + 2

@@ -270,7 +270,7 @@ def tile_gemma2attention_pa_kernel(tc, x, Wq, Wk, out_0, out_1):
         make_table(2, 1, 2)
         for t in (6, 7):
             bring_x(t)
-        group_w(1, 0, "scalar", heads=(1,))
+        group_w(1, 0, "scalar")
         group_w(1, 1, "scalar")
         for c in range(PASSES):
             group_w(2, c, "scalar")
@@ -289,7 +289,7 @@ def tile_gemma2attention_pa_kernel(tc, x, Wq, Wk, out_0, out_1):
 
         for n in range(TILES):
             g, t = divmod(n, TOKEN_TILES)
-            project_up_to(n + LOOKAHEAD + 1 if g > 0 else n + 2)
+            project_up_to(n + LOOKAHEAD + 1 if g > 0 else n + 3)
             rotate(n)
 
             phase = n % TENSOR_ADD_EVERY
@@ -313,8 +313,6 @@ def tile_gemma2attention_pa_kernel(tc, x, Wq, Wk, out_0, out_1):
                 quantise_x_pair(pair)
                 x_ready[0] = 2 * pair + 2
                 project_up_to(n + 3)
-            if n == 1:
-                group_w(1, 0, "vector", heads=(0,))
             if g + 1 < GROUPS and t == (QUANTISE_SECOND_AFTER if g == 0 else QUANTISE_NEXT_AFTER):
                 quantise_w(g + 1)
                 groups_ready[0] = g + 2

@@ -294,10 +294,11 @@ def tile_gemma2attention_pa_kernel(tc, x, Wq, Wk, out_0, out_1):
 
             phase = n % TENSOR_ADD_EVERY
             if n == TILES - 1:
-                add_and_store(n - 1, 1, "vector")
                 add_and_store(n, 1, "vector")
-            elif n == TILES - 2:
-                pass
+            elif n >= TILES - 3:
+                add_and_store(n, 1, "gpsimd")
+            elif n == TILES - 4:
+                add_and_store(n, 1, "tensor")
             elif n < FIRST_TENSOR_ADD - 1:
                 if n % 2 == 1:
                     add_and_store(n - 1, 2, "gpsimd")

@@ -30,6 +30,8 @@ FLOPS = 2 * TOKENS * K_DIM * GROUPS * GROUP_COLS
 
 TABLE_CHUNKS = [(0, 2), (2, 4), (4, 8)]
 
+REDUCED_PAIRS = 84
+
 LOOKAHEAD = 4
 TENSOR_ADD_EVERY = 4
 FIRST_TENSOR_ADD = 5
@@ -51,7 +53,6 @@ def tile_gemma2attention_pa_kernel(tc, x, Wq, Wk, out_0, out_1):
         x_raw = {}
         w_raw = {}
         turns = {}
-        reduced = {}
         tables = {}
         tables_q = {}
         x_turned = {}
@@ -90,27 +91,24 @@ def tile_gemma2attention_pa_kernel(tc, x, Wq, Wk, out_0, out_1):
             ratio = 10000.0 ** (-1.0 / HALF)
             k = 1
             while k < HALF:
-                nc.vector.tensor_scalar(out=angle[:, :, k:2 * k], in0=angle[:, :, 0:k], scalar1=ratio ** k,
-                                        scalar2=None, op0=ALU.mult)
-                k *= 2
+                for m in range(1, min(4, HALF // k)):
+                    nc.vector.tensor_scalar(out=angle[:, :, m * k:(m + 1) * k], in0=angle[:, :, 0:k],
+                                            scalar1=ratio ** (m * k), scalar2=None, op0=ALU.mult)
+                k *= 4
 
         def count_turns(key, t0, t1):
-            turns[key] = keep.tile([P, t1 - t0, HALF], I32, name="turns%d" % key)
-            nc.vector.tensor_scalar(out=turns[key][:], in0=angle[:, t0:t1, :], scalar1=1.0 / (2.0 * math.pi),
+            turns[key] = keep.tile([P, t1 - t0, REDUCED_PAIRS], I32, name="turns%d" % key)
+            nc.vector.tensor_scalar(out=turns[key][:], in0=angle[:, t0:t1, 0:REDUCED_PAIRS], scalar1=1.0 / (2.0 * math.pi),
                                     scalar2=None, op0=ALU.mult)
 
         def reduce_angles(key, t0, t1):
-            part = angle[:, t0:t1, :]
-            reduced[key] = keep.tile([P, t1 - t0, HALF], F32, name="reduced%d" % key)
-            nc.vector.scalar_tensor_tensor(out=reduced[key][:].rearrange("p t i -> p (t i)"),
-                                           in0=turns[key][:].rearrange("p t i -> p (t i)"),
-                                           scalar=-2.0 * math.pi,
-                                           in1=part.rearrange("p t i -> p (t i)"),
+            part = angle[:, t0:t1, 0:REDUCED_PAIRS]
+            nc.vector.scalar_tensor_tensor(out=part, in0=turns[key][:], scalar=-2.0 * math.pi, in1=part,
                                            op0=ALU.mult, op1=ALU.add)
 
-        def make_table(chunk, key, offset):
+        def make_table(chunk):
             count = TABLE_CHUNKS[chunk][1] - TABLE_CHUNKS[chunk][0]
-            part = reduced[key][:, offset:offset + count, :]
+            part = angle[:, TABLE_CHUNKS[chunk][0]:TABLE_CHUNKS[chunk][1], :]
             tables[chunk] = keep.tile([P, 2, count, 2, HALF], F32, name="table%d" % chunk)
             magnitude = keep.tile([P, count, HALF], F32, name="magnitude%d" % chunk)
             nc.scalar.activation(out=tables[chunk][:, 1, :, 0, :], in_=part, func=ACT.Sin)
@@ -249,25 +247,28 @@ def tile_gemma2attention_pa_kernel(tc, x, Wq, Wk, out_0, out_1):
                 load_w(g, c)
 
         make_angles()
-        group_w(0, 0, "vector", heads=(0,))
         count_turns(0, 0, 2)
-        group_w(0, 0, "vector", heads=(1,))
+        count_turns(1, 2, 8)
         reduce_angles(0, 0, 2)
+        reduce_angles(1, 2, 8)
+        make_table(0)
+        group_w(0, 0, "vector", heads=(0,))
+        group_w(0, 0, "vector", heads=(1,))
         bring_x(0)
-        make_table(0, 0, 0)
-        group_w(0, 1, "vector")
-        for t in (1, 2, 3, 4, 5):
-            bring_x(t)
+        make_table(1)
+        group_w(0, 1, "vector", heads=(0,))
         quantise_w_pass(0, 0)
+        group_w(0, 1, "vector", heads=(1,))
+        for t in (1, 2, 3):
+            bring_x(t)
         quantise_x(0)
         quantise_w_pass(0, 1)
         project(0)
-        count_turns(1, 2, 8)
+        for t in (4, 5):
+            bring_x(t)
         quantise_x(1)
-        reduce_angles(1, 2, 8)
         project(1)
-        make_table(1, 1, 0)
-        make_table(2, 1, 2)
+        make_table(2)
         for t in (6, 7):
             bring_x(t)
         group_w(1, 0, "scalar")

@@ -37,6 +37,8 @@ TENSOR_ADD_EVERY = 4
 FIRST_TENSOR_ADD = 5
 QUANTISE_NEXT_AFTER = 3
 QUANTISE_SECOND_AFTER = 6
+GPSIMD_PRODUCT_TILES = (33,)
+GPSIMD_LEAD = 5
 
 
 def tile_gemma2attention_pa_kernel(tc, x, Wq, Wk, out_0, out_1):
@@ -65,6 +67,8 @@ def tile_gemma2attention_pa_kernel(tc, x, Wq, Wk, out_0, out_1):
         sums = {}
         products = {}
         result = {}
+        sums_copy = {}
+        own_products = {}
 
         def load_x(t):
             x_raw[t] = keep.tile([P, K_DIM], BF16, name="x_raw%d" % t)
@@ -217,6 +221,21 @@ def tile_gemma2attention_pa_kernel(tc, x, Wq, Wk, out_0, out_1):
                 in1=table[:, :, row, :, :].rearrange("p e f i -> p (f i) e").unsqueeze(1).to_broadcast(shape),
                 op=ALU.mult)
 
+        def copy_sums(n):
+            sums_copy[n] = stage.tile([P, GROUP_COLS], F32, tag="sums_copy", bufs=1, name="sums_copy")
+            nc.scalar.copy(out=sums_copy[n][:], in_=sums[n][:])
+
+        def rotate_on_gpsimd(n):
+            g, t = divmod(n, TOKEN_TILES)
+            table, row = table_of(t, groups[g][3])
+            own_products[n] = stage.tile([P, GROUP_HEADS, 2, HEAD], F32, tag="own_products", bufs=1, name="own_products")
+            shape = [P, GROUP_HEADS, HEAD, 2]
+            nc.gpsimd.tensor_tensor(
+                out=own_products[n][:].rearrange("p h f (i e) -> p h (f i) e", e=2),
+                in0=sums_copy[n][:].rearrange("p (h m) -> p h m", h=GROUP_HEADS).unsqueeze(3).to_broadcast(shape),
+                in1=table[:, :, row, :, :].rearrange("p e f i -> p (f i) e").unsqueeze(1).to_broadcast(shape),
+                op=ALU.mult)
+
         def add_and_store(n, count, engine):
             g, t = divmod(n, TOKEN_TILES)
             target, h0 = groups[g][1], groups[g][2]
@@ -230,8 +249,9 @@ def tile_gemma2attention_pa_kernel(tc, x, Wq, Wk, out_0, out_1):
                 nc.gpsimd.tensor_tensor(out=r, in0=a, in1=b, op=ALU.add)
             else:
                 total = psum.tile([P, GROUP_HEADS, HEAD], F32, tag="bank", name="total")
-                nc.tensor.matmul(out=total[:], lhsT=identity[:], rhs=products[pair][:, slot, :, 0, :], start=True, stop=False)
-                nc.tensor.matmul(out=total[:], lhsT=identity[:], rhs=products[pair][:, slot, :, 1, :], start=False, stop=True)
+                made = own_products[n][:] if n in own_products else products[pair][:, slot, :, :, :]
+                nc.tensor.matmul(out=total[:], lhsT=identity[:], rhs=made[:, :, 0, :], start=True, stop=False)
+                nc.tensor.matmul(out=total[:], lhsT=identity[:], rhs=made[:, :, 1, :], start=False, stop=True)
                 nc.scalar.copy(out=result[pair][:, slot, :], in_=total[:].rearrange("p h d -> p (h d)"))
             nc.sync.dma_start(
                 out=target[0, t * P:(t + count) * P, h0:h0 + GROUP_HEADS, :].rearrange("(a p) h d -> p a h d", p=P),
@@ -277,6 +297,7 @@ def tile_gemma2attention_pa_kernel(tc, x, Wq, Wk, out_0, out_1):
             group_w(2, c, "scalar")
         make_tables_q()
 
+        late_w = []
         projected = [2]
         x_ready = [2]
         groups_ready = [1]
@@ -285,13 +306,21 @@ def tile_gemma2attention_pa_kernel(tc, x, Wq, Wk, out_0, out_1):
             while projected[0] < min(limit, TILES, groups_ready[0] * TOKEN_TILES):
                 if projected[0] < TOKEN_TILES and projected[0] >= x_ready[0]:
                     break
-                project(projected[0])
+                if projected[0] not in sums:
+                    project(projected[0])
                 projected[0] += 1
 
         for n in range(TILES):
             g, t = divmod(n, TOKEN_TILES)
             project_up_to(n + LOOKAHEAD + 1 if g > 0 else n + 3)
-            rotate(n)
+            if n + GPSIMD_LEAD in GPSIMD_PRODUCT_TILES:
+                project(n + GPSIMD_LEAD)
+                copy_sums(n + GPSIMD_LEAD)
+            if late_w:
+                group_w(late_w[0], 1, "scalar")
+                late_w.clear()
+            if n not in GPSIMD_PRODUCT_TILES:
+                rotate(n)
 
             phase = n % TENSOR_ADD_EVERY
             if n == TILES - 1:
@@ -310,6 +339,9 @@ def tile_gemma2attention_pa_kernel(tc, x, Wq, Wk, out_0, out_1):
             elif phase == 3:
                 add_and_store(n - 1, 2, "gpsimd")
 
+            if n + GPSIMD_LEAD in GPSIMD_PRODUCT_TILES:
+                rotate_on_gpsimd(n + GPSIMD_LEAD)
+
             if g == 0 and t in (0, 1, 3):
                 pair = (1, 2, 0, 3)[t]
                 quantise_x_pair(pair)
@@ -319,6 +351,6 @@ def tile_gemma2attention_pa_kernel(tc, x, Wq, Wk, out_0, out_1):
                 quantise_w(g + 1)
                 groups_ready[0] = g + 2
                 if g + 3 < GROUPS:
-                    for c in range(PASSES):
-                        group_w(g + 3, c, "scalar")
+                    group_w(g + 3, 0, "scalar")
+                    late_w.append(g + 3)
                 project_up_to(n + LOOKAHEAD + 1)

import math
from contextlib import ExitStack

import concourse.mybir as mybir
from concourse.masks import make_identity

F32 = mybir.dt.float32
BF16 = mybir.dt.bfloat16
U32 = mybir.dt.uint32
U8 = mybir.dt.uint8
I32 = mybir.dt.int32
FP8X4 = mybir.dt.float8_e5m2_x4
ALU = mybir.AluOpType
ACT = mybir.ActivationFunctionType

P = 128
TOKENS = 1024
K_DIM = 1024
HEAD = 256
HALF = HEAD // 2
PACK = 4
K_PASS = P * PACK
PASSES = K_DIM // K_PASS
TOKEN_TILES = TOKENS // P
GROUP_HEADS = 2
GROUP_COLS = GROUP_HEADS * HEAD
GROUPS = 6
TILES = GROUPS * TOKEN_TILES
FLOPS = 2 * TOKENS * K_DIM * GROUPS * GROUP_COLS

TABLE_CHUNKS = [(0, 2), (2, 4), (4, 8)]

REDUCED_PAIRS = 84

LOOKAHEAD = 4
TENSOR_ADD_EVERY = 4
FIRST_TENSOR_ADD = 5
QUANTISE_NEXT_AFTER = 3
QUANTISE_SECOND_AFTER = 6
GPSIMD_PRODUCT_TILES = (33,)
GPSIMD_LEAD = 5


def tile_gemma2attention_pa_kernel(tc, x, Wq, Wk, out_0, out_1):
    nc = tc.nc
    groups = [(Wk, out_1, 0, False), (Wk, out_1, 2, False),
              (Wq, out_0, 0, True), (Wq, out_0, 2, True), (Wq, out_0, 4, True), (Wq, out_0, 6, True)]

    with ExitStack() as ctx:
        keep = ctx.enter_context(tc.tile_pool(name="keep", bufs=1))
        stage = ctx.enter_context(tc.tile_pool(name="stage", bufs=4))
        psum = ctx.enter_context(tc.psum_pool(name="psum", bufs=8))
        ctx.enter_context(tc.manual_schedule())

        x_raw = {}
        w_raw = {}
        turns = {}
        tables = {}
        tables_q = {}
        x_turned = {}
        x_grouped = {}
        x_codes = {}
        x_scales = {}
        w_grouped = {}
        w_codes = {}
        w_scales = {}
        sums = {}
        products = {}
        result = {}
        sums_copy = {}
        own_products = {}

        def load_x(t):
            x_raw[t] = keep.tile([P, K_DIM], BF16, name="x_raw%d" % t)
            nc.sync.dma_start(out=x_raw[t][:], in_=x[0, t * P:(t + 1) * P, :])

        def load_w(g, c):
            weights, h0 = groups[g][0], groups[g][2]
            w_raw[(g, c)] = keep.tile([P, GROUP_HEADS, PACK, HEAD], BF16, name="w_raw%d_%d" % (g, c))
            nc.sync.dma_start(
                out=w_raw[(g, c)][:],
                in_=weights[h0:h0 + GROUP_HEADS, c * K_PASS:(c + 1) * K_PASS, :].rearrange(
                    "h (p j) w -> p h j w", j=PACK))

        angle = keep.tile([P, TOKEN_TILES, HALF], F32, name="angle")
        identity = keep.tile([P, P], F32, name="identity")
        warm = keep.tile([P, 2], F32, name="warm")

        def make_angles():
            nc.gpsimd.iota(angle[:, :, 0], pattern=[[P, TOKEN_TILES]], base=0, channel_multiplier=1,
                           allow_small_or_imprecise_dtypes=True)
            make_identity(nc, identity[:])
            nc.vector.memset(warm[:, 0:1], 0.0)
            nc.scalar.activation(out=warm[:, 1:2], in_=warm[:, 0:1], func=ACT.Sin)
            ratio = 10000.0 ** (-1.0 / HALF)
            k = 1
            while k < HALF:
                for m in range(1, min(4, HALF // k)):
                    nc.vector.tensor_scalar(out=angle[:, :, m * k:(m + 1) * k], in0=angle[:, :, 0:k],
                                            scalar1=ratio ** (m * k), scalar2=None, op0=ALU.mult)
                k *= 4

        def count_turns(key, t0, t1):
            turns[key] = keep.tile([P, t1 - t0, REDUCED_PAIRS], I32, name="turns%d" % key)
            nc.vector.tensor_scalar(out=turns[key][:], in0=angle[:, t0:t1, 0:REDUCED_PAIRS], scalar1=1.0 / (2.0 * math.pi),
                                    scalar2=None, op0=ALU.mult)

        def reduce_angles(key, t0, t1):
            part = angle[:, t0:t1, 0:REDUCED_PAIRS]
            nc.vector.scalar_tensor_tensor(out=part, in0=turns[key][:], scalar=-2.0 * math.pi, in1=part,
                                           op0=ALU.mult, op1=ALU.add)

        def make_table(chunk):
            count = TABLE_CHUNKS[chunk][1] - TABLE_CHUNKS[chunk][0]
            part = angle[:, TABLE_CHUNKS[chunk][0]:TABLE_CHUNKS[chunk][1], :]
            tables[chunk] = keep.tile([P, 2, count, 2, HALF], F32, name="table%d" % chunk)
            magnitude = keep.tile([P, count, HALF], F32, name="magnitude%d" % chunk)
            nc.scalar.activation(out=tables[chunk][:, 1, :, 0, :], in_=part, func=ACT.Sin)
            nc.scalar.activation(out=magnitude[:], in_=part, func=ACT.Abs)
            nc.scalar.activation(out=tables[chunk][:, 0, :, 0, :], in_=magnitude[:], func=ACT.Sin,
                                 scale=-1.0, bias=math.pi / 2.0)
            nc.gpsimd.tensor_scalar(out=tables[chunk][:, 0, :, 1, :], in0=tables[chunk][:, 1, :, 0, :],
                                    scalar1=-1.0, scalar2=0.0, op0=ALU.mult, op1=ALU.add)
            nc.gpsimd.tensor_scalar(out=tables[chunk][:, 1, :, 1, :], in0=tables[chunk][:, 0, :, 0, :],
                                    scalar1=1.0, scalar2=0.0, op0=ALU.mult, op1=ALU.add)

        def make_tables_q():
            for chunk in range(len(TABLE_CHUNKS)):
                count = TABLE_CHUNKS[chunk][1] - TABLE_CHUNKS[chunk][0]
                tables_q[chunk] = keep.tile([P, 2, count, 2, HALF], F32, name="table_q%d" % chunk)
                nc.scalar.activation(out=tables_q[chunk][:].rearrange("p e t f i -> p (e t f i)"),
                                     in_=tables[chunk][:].rearrange("p e t f i -> p (e t f i)"), func=ACT.Copy, scale=1.0 / 16.0)

        def table_of(t, divided):
            for chunk in range(len(TABLE_CHUNKS)):
                t0, t1 = TABLE_CHUNKS[chunk]
                if t0 <= t < t1:
                    return (tables_q[chunk] if divided else tables[chunk]), t - t0
            raise ValueError("no table for token tile %d" % t)

        def turn_x(t):
            words = x_raw[t][:].bitcast(F32)
            x_turned[t] = psum.tile([P, PASSES, 2, P], F32, tag="bank", name="x_turned")
            for c in range(PASSES):
                for u in range(2):
                    nc.tensor.transpose(x_turned[t][:, c, u, :], words[:, 256 * c + u:256 * (c + 1):2],
                                        identity[:])

        def group_x(t):
            pair, slot = divmod(t, 2)
            if slot == 0:
                x_grouped[pair] = stage.tile([P, 2, PASSES * P * PACK], BF16, tag="x_grouped", bufs=4,
                                             name="x_grouped", align_bytes=64)
                x_codes[pair] = keep.tile([P, 2, PASSES * P], U32, name="x_codes%d" % pair, align_bytes=64)
                x_scales[pair] = keep.tile([P, 2, PASSES * P], U8, name="x_scales%d" % pair, align_bytes=64)
            nc.scalar.copy(
                out=x_grouped[pair][:, slot, :].bitcast(F32).rearrange("p (c r u) -> p c r u", c=PASSES, u=2),
                in_=x_turned[t][:].rearrange("p c u r -> p c r u"))

        def bring_x(t):
            turn_x(t)
            group_x(t)

        def quantise_x(t):
            pair, slot = divmod(t, 2)
            nc.vector.quantize_mx(out=x_codes[pair][:, slot, :].bitcast(FP8X4), scales=x_scales[pair][:, slot, :],
                                  in_=x_grouped[pair][:, slot, :])

        def quantise_x_pair(pair):
            nc.vector.quantize_mx(out=x_codes[pair][:].rearrange("p a n -> p (a n)").bitcast(FP8X4),
                                  scales=x_scales[pair][:].rearrange("p a n -> p (a n)"),
                                  in_=x_grouped[pair][:].rearrange("p a n -> p (a n)"))

        def group_w(g, c, engine, heads=(0, 1)):
            if g not in w_grouped:
                w_grouped[g] = stage.tile([P, PASSES, GROUP_COLS * PACK], BF16, tag="w_grouped", bufs=3,
                                          name="w_grouped", align_bytes=64)
                w_codes[g] = keep.tile([P, PASSES, GROUP_COLS], U32, name="w_codes%d" % g, align_bytes=64)
                w_scales[g] = keep.tile([P, PASSES, GROUP_COLS], U8, name="w_scales%d" % g, align_bytes=64)
            for h in heads:
                target = w_grouped[g][:, c, h * HEAD * PACK:(h + 1) * HEAD * PACK].rearrange(
                    "p (q i j) -> p q j i", i=4, j=PACK)
                source = w_raw[(g, c)][:, h, :, :].rearrange("p j (q i) -> p q j i", i=4)
                if engine == "vector":
                    nc.vector.tensor_copy(out=target, in_=source)
                else:
                    nc.scalar.copy(out=target, in_=source)

        def quantise_w_pass(g, c):
            nc.vector.quantize_mx(out=w_codes[g][:, c, :].bitcast(FP8X4), scales=w_scales[g][:, c, :],
                                  in_=w_grouped[g][:, c, :])

        def quantise_w(g):
            nc.vector.quantize_mx(out=w_codes[g][:].rearrange("p c n -> p (c n)").bitcast(FP8X4),
                                  scales=w_scales[g][:].rearrange("p c n -> p (c n)"),
                                  in_=w_grouped[g][:].rearrange("p c n -> p (c n)"))

        def project(n):
            g, t = divmod(n, TOKEN_TILES)
            pair, slot = divmod(t, 2)
            sums[n] = psum.tile([P, GROUP_COLS], F32, tag="bank", name="sums")
            for c in range(PASSES):
                nc.tensor.matmul_mx(out=sums[n][:],
                                    lhsT=x_codes[pair][:, slot, c * P:(c + 1) * P].bitcast(FP8X4),
                                    lhsT_scale=x_scales[pair][:, slot, c * P:(c + 1) * P],
                                    rhs=w_codes[g][:, c, :].bitcast(FP8X4),
                                    rhs_scale=w_scales[g][:, c, :],
                                    start=(c == 0), stop=(c == PASSES - 1))

        def rotate(n):
            g, t = divmod(n, TOKEN_TILES)
            table, row = table_of(t, groups[g][3])
            pair, slot = divmod(n, 2)
            if slot == 0:
                products[pair] = stage.tile([P, 2, GROUP_HEADS, 2, HEAD], F32, tag="products", bufs=3, name="products")
                result[pair] = stage.tile([P, 2, GROUP_COLS], F32, tag="result", bufs=4, name="result")
            shape = [P, GROUP_HEADS, HEAD, 2]
            nc.vector.tensor_tensor(
                out=products[pair][:, slot, :, :, :].rearrange("p h f (i e) -> p h (f i) e", e=2),
                in0=sums[n][:].rearrange("p (h m) -> p h m", h=GROUP_HEADS).unsqueeze(3).to_broadcast(shape),
                in1=table[:, :, row, :, :].rearrange("p e f i -> p (f i) e").unsqueeze(1).to_broadcast(shape),
                op=ALU.mult)

        def copy_sums(n):
            sums_copy[n] = stage.tile([P, GROUP_COLS], F32, tag="sums_copy", bufs=1, name="sums_copy")
            nc.scalar.copy(out=sums_copy[n][:], in_=sums[n][:])

        def rotate_on_gpsimd(n):
            g, t = divmod(n, TOKEN_TILES)
            table, row = table_of(t, groups[g][3])
            own_products[n] = stage.tile([P, GROUP_HEADS, 2, HEAD], F32, tag="own_products", bufs=1, name="own_products")
            shape = [P, GROUP_HEADS, HEAD, 2]
            nc.gpsimd.tensor_tensor(
                out=own_products[n][:].rearrange("p h f (i e) -> p h (f i) e", e=2),
                in0=sums_copy[n][:].rearrange("p (h m) -> p h m", h=GROUP_HEADS).unsqueeze(3).to_broadcast(shape),
                in1=table[:, :, row, :, :].rearrange("p e f i -> p (f i) e").unsqueeze(1).to_broadcast(shape),
                op=ALU.mult)

        def add_and_store(n, count, engine):
            g, t = divmod(n, TOKEN_TILES)
            target, h0 = groups[g][1], groups[g][2]
            pair, slot = divmod(n, 2)
            a = products[pair][:, slot:slot + count, :, 0, :]
            b = products[pair][:, slot:slot + count, :, 1, :]
            r = result[pair][:, slot:slot + count, :].rearrange("p a (h d) -> p a h d", h=GROUP_HEADS)
            if engine == "vector":
                nc.vector.tensor_tensor(out=r, in0=a, in1=b, op=ALU.add)
            elif engine == "gpsimd":
                nc.gpsimd.tensor_tensor(out=r, in0=a, in1=b, op=ALU.add)
            else:
                total = psum.tile([P, GROUP_HEADS, HEAD], F32, tag="bank", name="total")
                made = own_products[n][:] if n in own_products else products[pair][:, slot, :, :, :]
                nc.tensor.matmul(out=total[:], lhsT=identity[:], rhs=made[:, :, 0, :], start=True, stop=False)
                nc.tensor.matmul(out=total[:], lhsT=identity[:], rhs=made[:, :, 1, :], start=False, stop=True)
                nc.scalar.copy(out=result[pair][:, slot, :], in_=total[:].rearrange("p h d -> p (h d)"))
            nc.sync.dma_start(
                out=target[0, t * P:(t + count) * P, h0:h0 + GROUP_HEADS, :].rearrange("(a p) h d -> p a h d", p=P),
                in_=r)

        load_w(0, 0)
        load_x(0)
        load_w(0, 1)
        for t in range(1, TOKEN_TILES):
            load_x(t)
        for g in range(1, GROUPS):
            for c in range(PASSES):
                load_w(g, c)

        make_angles()
        count_turns(0, 0, 2)
        count_turns(1, 2, 8)
        reduce_angles(0, 0, 2)
        reduce_angles(1, 2, 8)
        make_table(0)
        group_w(0, 0, "vector", heads=(0,))
        group_w(0, 0, "vector", heads=(1,))
        bring_x(0)
        make_table(1)
        group_w(0, 1, "vector", heads=(0,))
        quantise_w_pass(0, 0)
        group_w(0, 1, "vector", heads=(1,))
        for t in (1, 2, 3):
            bring_x(t)
        quantise_x(0)
        quantise_w_pass(0, 1)
        project(0)
        for t in (4, 5):
            bring_x(t)
        quantise_x(1)
        project(1)
        make_table(2)
        for t in (6, 7):
            bring_x(t)
        group_w(1, 0, "scalar")
        group_w(1, 1, "scalar")
        for c in range(PASSES):
            group_w(2, c, "scalar")
        make_tables_q()

        late_w = []
        projected = [2]
        x_ready = [2]
        groups_ready = [1]

        def project_up_to(limit):
            while projected[0] < min(limit, TILES, groups_ready[0] * TOKEN_TILES):
                if projected[0] < TOKEN_TILES and projected[0] >= x_ready[0]:
                    break
                if projected[0] not in sums:
                    project(projected[0])
                projected[0] += 1

        for n in range(TILES):
            g, t = divmod(n, TOKEN_TILES)
            project_up_to(n + LOOKAHEAD + 1 if g > 0 else n + 3)
            if n + GPSIMD_LEAD in GPSIMD_PRODUCT_TILES:
                project(n + GPSIMD_LEAD)
                copy_sums(n + GPSIMD_LEAD)
            if late_w:
                group_w(late_w[0], 1, "scalar")
                late_w.clear()
            if n not in GPSIMD_PRODUCT_TILES:
                rotate(n)

            phase = n % TENSOR_ADD_EVERY
            if n == TILES - 1:
                add_and_store(n, 1, "vector")
            elif n >= TILES - 3:
                add_and_store(n, 1, "gpsimd")
            elif n == TILES - 4:
                add_and_store(n, 1, "tensor")
            elif n < FIRST_TENSOR_ADD - 1:
                if n % 2 == 1:
                    add_and_store(n - 1, 2, "gpsimd")
            elif phase == 0:
                add_and_store(n, 1, "gpsimd")
            elif phase == 1:
                add_and_store(n, 1, "tensor")
            elif phase == 3:
                add_and_store(n - 1, 2, "gpsimd")

            if n + GPSIMD_LEAD in GPSIMD_PRODUCT_TILES:
                rotate_on_gpsimd(n + GPSIMD_LEAD)

            if g == 0 and t in (0, 1, 3):
                pair = (1, 2, 0, 3)[t]
                quantise_x_pair(pair)
                x_ready[0] = 2 * pair + 2
                project_up_to(n + 3)
            if g + 1 < GROUPS and t == (QUANTISE_SECOND_AFTER if g == 0 else QUANTISE_NEXT_AFTER):
                quantise_w(g + 1)
                groups_ready[0] = g + 2
                if g + 3 < GROUPS:
                    group_w(g + 3, 0, "scalar")
                    late_w.append(g + 3)
                project_up_to(n + LOOKAHEAD + 1)
